import numpy as np
import ml_dtypes


def mxq(x, axis, fmt="e4m3"):
    dtype, down = {"e4m3": (ml_dtypes.float8_e4m3fn, 7), "e5m2": (ml_dtypes.float8_e5m2, 14)}[fmt]
    v = np.moveaxis(np.asarray(x, np.float32).astype(ml_dtypes.bfloat16).astype(np.float64), axis, -1)
    blocks = v.reshape(v.shape[:-1] + (-1, 32))
    amax = np.abs(blocks).max(-1, keepdims=True)
    byte = np.maximum(np.where(amax > 0, np.frexp(amax)[1] - 1 + 127, 0) - down, 1)
    scale = np.exp2(byte - 127.0)
    codes = (blocks / scale).astype(np.float32).astype(dtype).astype(np.float64)
    return np.moveaxis((codes * scale).reshape(v.shape), -1, axis)


WIDE = False


def mx_kscale(k):
    if not WIDE:
        return np.ones(k)
    levels = np.array([10, -10, 5, -5, 0])
    a = np.random.permutation(np.resize(levels, k // 512 * 4)).reshape(k // 512, 4)
    idx = np.arange(k)
    return np.exp2(a[idx // 512, idx % 128 // 32])


BF16 = ml_dtypes.bfloat16


def bf(x):
    return np.asarray(x, np.float32).astype(BF16)


def f64(x):
    return np.asarray(x).astype(np.float64)


B, IN, OUT = 512, 2048, 1536

EPS = 1e-07


def sigmoid(v):
    return 1.0 / (1.0 + np.exp(-v))


def setup_inputs():
    s = mx_kscale(IN)
    u = s / s.min()
    return {"input_tensor": bf(np.random.standard_normal((B, IN)) * u),
            "W_hat": bf(np.random.standard_normal((IN, OUT)) * 1.0 / np.sqrt(IN) / u[:, None]),
            "M_hat": bf(np.random.standard_normal((IN, OUT)) * 1.0),
            "gate": bf(np.random.standard_normal((IN, OUT)) * 1.0 / np.sqrt(IN) / u[:, None])}


def reference(input_tensor, W_hat, M_hat, gate):
    x = f64(input_tensor)
    W = np.tanh(f64(W_hat)) * sigmoid(f64(M_hat))
    xq = mxq(x, 1, "e4m3")
    Wq = mxq(W, 0, "e4m3")
    a = xq @ Wq
    m = np.exp(mxq(np.log(np.abs(x) + EPS), 1, "e4m3") @ Wq)
    g = sigmoid(xq @ mxq(f64(gate), 0, "e4m3"))
    return g * a + (1.0 - g) * m

@@ -1,0 +1,145 @@
+from contextlib import ExitStack
+
+import concourse.mybir as mybir
+from concourse.masks import make_identity
+
+FP8X4 = mybir.dt.float8_e4m3fn_x4
+BF16 = mybir.dt.bfloat16
+F32 = mybir.dt.float32
+I32 = mybir.dt.int32
+U32 = mybir.dt.uint32
+U8 = mybir.dt.uint8
+ACT = mybir.ActivationFunctionType
+ALU = mybir.AluOpType
+
+P = 128
+PACK = 4
+K_PASS = P * PACK
+B, IN, OUT = 512, 2048, 1536
+PASSES = IN // K_PASS
+ROW_TILES = B // P
+RANGE = 512
+EPS = 1e-07
+FLOPS = 3 * 2 * B * IN * OUT
+
+
+def tile_nalu_kernel(tc, input_tensor, W_hat, M_hat, gate, out):
+    nc = tc.nc
+    with ExitStack() as ctx:
+        const = ctx.enter_context(tc.tile_pool(name="const", bufs=1))
+        keep = ctx.enter_context(tc.tile_pool(name="keep", bufs=1))
+        xin = ctx.enter_context(tc.tile_pool(name="xin", bufs=2))
+        raw = ctx.enter_context(tc.tile_pool(name="raw", bufs=3))
+        fac = ctx.enter_context(tc.tile_pool(name="fac", bufs=2))
+        grp = ctx.enter_context(tc.tile_pool(name="grp", bufs=2))
+        wq = ctx.enter_context(tc.tile_pool(name="wq", bufs=2))
+        epi = ctx.enter_context(tc.tile_pool(name="epi", bufs=2))
+        psum = ctx.enter_context(tc.psum_pool(name="psum", bufs=2))
+
+        ident = const.tile([P, P], F32)
+        make_identity(nc, ident[:])
+        eps = const.tile([P, 1], F32)
+        nc.vector.memset(eps[:], EPS)
+
+        x_codes = keep.tile([P, ROW_TILES, PASSES * P], U32, align_bytes=64)
+        x_scales = keep.tile([P, ROW_TILES, PASSES * P], U8, align_bytes=64)
+        l_codes = keep.tile([P, ROW_TILES, PASSES * P], U32, align_bytes=64)
+        l_scales = keep.tile([P, ROW_TILES, PASSES * P], U8, align_bytes=64)
+
+        for i in range(ROW_TILES):
+            x_sb = xin.tile([P, IN], BF16)
+            nc.sync.dma_start(out=x_sb[:], in_=input_tensor[i * P : (i + 1) * P, :])
+            words = x_sb[:].bitcast(F32)
+            xg = xin.tile([P, PASSES * P * PACK], BF16, align_bytes=64)
+            xg_words = xg[:].bitcast(F32).rearrange("p (c r u) -> p c r u", c=PASSES, u=2)
+            for half in range(PASSES // 2):
+                xt = psum.tile([P, 2, 2, P], F32, tag="xt")
+                for c2 in range(2):
+                    c = 2 * half + c2
+                    for u in range(2):
+                        nc.tensor.transpose(xt[:, c2, u, :], words[:, 256 * c + u : 256 * (c + 1) : 2], ident[:])
+                nc.vector.tensor_copy(
+                    out=xg_words[:, 2 * half : 2 * half + 2], in_=xt[:].rearrange("p c u r -> p c r u")
+                )
+            xa = xin.tile([P, PASSES * P * PACK], BF16)
+            nc.vector.tensor_single_scalar(
+                out=xa[:].bitcast(I32), in_=xg[:].bitcast(I32), scalar=0x7FFF7FFF, op=ALU.bitwise_and
+            )
+            lg = xin.tile([P, PASSES * P * PACK], BF16, align_bytes=64)
+            nc.scalar.activation(out=lg[:], in_=xa[:], func=ACT.Ln, bias=eps[:], scale=1.0)
+            nc.vector.quantize_mx(out=x_codes[:, i, :].bitcast(FP8X4), scales=x_scales[:, i, :], in_=xg[:])
+            nc.vector.quantize_mx(out=l_codes[:, i, :].bitcast(FP8X4), scales=l_scales[:, i, :], in_=lg[:])
+
+        def load(src, c, n0, tag):
+            rows = raw.tile([P, PACK, RANGE], BF16, tag=tag, name=tag)
+            nc.sync.dma_start(
+                out=rows[:],
+                in_=src[c * K_PASS : (c + 1) * K_PASS, n0 : n0 + RANGE].rearrange("(p t) n -> p t n", t=PACK),
+            )
+            return rows
+
+        def by_runs(rows):
+            return rows[:].rearrange("p t (c i) -> p c t i", i=4)
+
+        def grouped(tile_):
+            return tile_[:].rearrange("p (c i) t -> p c t i", i=4)
+
+        def product(acc, lhs_codes, lhs_scales, i, rhs_codes, rhs_scales):
+            for c in range(PASSES):
+                nc.tensor.matmul_mx(
+                    out=acc[:],
+                    lhsT=lhs_codes[:, i, c * P : (c + 1) * P].bitcast(FP8X4),
+                    lhsT_scale=lhs_scales[:, i, c * P : (c + 1) * P],
+                    rhs=rhs_codes[:, c, :].bitcast(FP8X4),
+                    rhs_scale=rhs_scales[:, c, :],
+                    start=(c == 0),
+                    stop=(c == PASSES - 1),
+                )
+
+        for n0 in range(0, OUT, RANGE):
+            w_codes = wq.tile([P, PASSES, RANGE], U32, align_bytes=64)
+            w_scales = wq.tile([P, PASSES, RANGE], U8, align_bytes=64)
+            g_codes = wq.tile([P, PASSES, RANGE], U32, align_bytes=64)
+            g_scales = wq.tile([P, PASSES, RANGE], U8, align_bytes=64)
+            for c in range(PASSES):
+                gr = load(gate, c, n0, "gr")
+                gg = grp.tile([P, RANGE, PACK], BF16, align_bytes=64)
+                nc.vector.tensor_copy(out=grouped(gg), in_=by_runs(gr))
+                wh = load(W_hat, c, n0, "wh")
+                mh = load(M_hat, c, n0, "mh")
+                t1 = fac.tile([P, RANGE, PACK], F32)
+                nc.scalar.activation(out=grouped(t1), in_=by_runs(wh), func=ACT.Tanh)
+                t2 = fac.tile([P, RANGE, PACK], F32)
+                nc.scalar.activation(out=grouped(t2), in_=by_runs(mh), func=ACT.Tanh, scale=0.5)
+                nc.vector.quantize_mx(
+                    out=g_codes[:, c, :].bitcast(FP8X4), scales=g_scales[:, c, :], in_=gg[:].rearrange("p n t -> p (n t)")
+                )
+                wg = grp.tile([P, RANGE * PACK], BF16, align_bytes=64)
+                nc.vector.scalar_tensor_tensor(
+                    out=wg[:],
+                    in0=t2[:].rearrange("p n t -> p (n t)"),
+                    scalar=1.0,
+                    in1=t1[:].rearrange("p n t -> p (n t)"),
+                    op0=ALU.add,
+                    op1=ALU.mult,
+                )
+                nc.vector.quantize_mx(out=w_codes[:, c, :].bitcast(FP8X4), scales=w_scales[:, c, :], in_=wg[:])
+
+            for i in range(ROW_TILES):
+                z = psum.tile([P, RANGE], F32, tag="z")
+                product(z, x_codes, x_scales, i, g_codes, g_scales)
+                a2 = psum.tile([P, RANGE], F32, tag="a2")
+                product(a2, x_codes, x_scales, i, w_codes, w_scales)
+                s2 = psum.tile([P, RANGE], F32, tag="s2")
+                product(s2, l_codes, l_scales, i, w_codes, w_scales)
+                th = epi.tile([P, RANGE], F32)
+                nc.scalar.activation(out=th[:], in_=z[:], func=ACT.Tanh, scale=0.5)
+                m = epi.tile([P, RANGE], F32)
+                nc.scalar.activation(out=m[:], in_=s2[:], func=ACT.Exp, scale=0.5)
+                d = epi.tile([P, RANGE], F32)
+                nc.vector.scalar_tensor_tensor(out=d[:], in0=a2[:], scalar=0.5, in1=m[:], op0=ALU.mult, op1=ALU.subtract)
+                e = epi.tile([P, RANGE], F32)
+                nc.vector.scalar_tensor_tensor(out=e[:], in0=th[:], scalar=1.0, in1=d[:], op0=ALU.add, op1=ALU.mult)
+                o = epi.tile([P, RANGE], F32)
+                nc.vector.scalar_tensor_tensor(out=o[:], in0=e[:], scalar=0.5, in1=m[:], op0=ALU.mult, op1=ALU.add)
+                nc.sync.dma_start(out=out[i * P : (i + 1) * P, n0 : n0 + RANGE], in_=o[:])

@@ -18,23 +18,51 @@ K_PASS = P * PACK
 B, IN, OUT = 512, 2048, 1536
 PASSES = IN // K_PASS
 ROW_TILES = B // P
-RANGE = 512
+CHUNK = 512
 EPS = 1e-07
 FLOPS = 3 * 2 * B * IN * OUT
+
+RANGES = ((0, 512), (512, 512), (1024, 256), (1280, 128), (1408, 128))
+RAW_BUFS = 4
+PINNED = True
+GATE_SLOTS = {2: (4, 5), 3: (6,), 4: (7, 8), 5: (9,), 6: (10,), 7: (11,)}
+TH_AFTER_W = {3: (0,), 4: (2,), 7: (4,), 8: (6,), 9: (8,)}
+TH_AFTER_M = {3: (1,), 4: (3,), 7: (5,), 8: (7,), 9: (9,), 11: (10, 11)}
+EX_AFTER_W = {5: (0,), 6: (2,), 9: (4,), 10: (6,), 11: (8,)}
+EX_AFTER_M = {5: (1,), 6: (3,), 9: (5,), 10: (7,), 11: (9,)}
 
 
 def tile_nalu_kernel(tc, input_tensor, W_hat, M_hat, gate, out):
     nc = tc.nc
+    chunks = []
+    units = []
+    last_chunk = []
+    for r, (n0, width) in enumerate(RANGES):
+        per = CHUNK // width
+        for c0 in range(0, PASSES, per):
+            chunks.append((r, tuple(range(c0, c0 + per))))
+        last_chunk.append(len(chunks) - 1)
+        for i0 in range(0, ROW_TILES, per):
+            units.append((r, tuple(range(i0, i0 + per))))
+    first_chunk = [last_chunk[r] + 1 - PASSES * RANGES[r][1] // CHUNK for r in range(len(RANGES))]
+
     with ExitStack() as ctx:
         const = ctx.enter_context(tc.tile_pool(name="const", bufs=1))
         keep = ctx.enter_context(tc.tile_pool(name="keep", bufs=1))
-        xin = ctx.enter_context(tc.tile_pool(name="xin", bufs=2))
-        raw = ctx.enter_context(tc.tile_pool(name="raw", bufs=3))
+        xin = ctx.enter_context(tc.tile_pool(name="xin", bufs=3))
+        xwork = ctx.enter_context(tc.tile_pool(name="xwork", bufs=4))
+        lwork = ctx.enter_context(tc.tile_pool(name="lwork", bufs=4))
+        raw = ctx.enter_context(tc.tile_pool(name="raw", bufs=RAW_BUFS))
         fac = ctx.enter_context(tc.tile_pool(name="fac", bufs=2))
         grp = ctx.enter_context(tc.tile_pool(name="grp", bufs=2))
-        wq = ctx.enter_context(tc.tile_pool(name="wq", bufs=2))
-        epi = ctx.enter_context(tc.tile_pool(name="epi", bufs=2))
-        psum = ctx.enter_context(tc.psum_pool(name="psum", bufs=2))
+        wq = ctx.enter_context(tc.tile_pool(name="wq", bufs=9))
+        gq = ctx.enter_context(tc.tile_pool(name="gq", bufs=8))
+        epi = ctx.enter_context(tc.tile_pool(name="epi", bufs=3))
+        gates = ctx.enter_context(tc.tile_pool(name="gates", bufs=6))
+        psz = ctx.enter_context(tc.psum_pool(name="psz", bufs=2))
+        psa = ctx.enter_context(tc.psum_pool(name="psa", bufs=3))
+        if PINNED:
+            ctx.enter_context(tc.manual_schedule())
 
         ident = const.tile([P, P], F32)
         make_identity(nc, ident[:])
@@ -46,14 +74,43 @@ def tile_nalu_kernel(tc, input_tensor, W_hat, M_hat, gate, out):
         l_codes = keep.tile([P, ROW_TILES, PASSES * P], U32, align_bytes=64)
         l_scales = keep.tile([P, ROW_TILES, PASSES * P], U8, align_bytes=64)
 
-        for i in range(ROW_TILES):
-            x_sb = xin.tile([P, IN], BF16)
-            nc.sync.dma_start(out=x_sb[:], in_=input_tensor[i * P : (i + 1) * P, :])
-            words = x_sb[:].bitcast(F32)
-            xg = xin.tile([P, PASSES * P * PACK], BF16, align_bytes=64)
-            xg_words = xg[:].bitcast(F32).rearrange("p (c r u) -> p c r u", c=PASSES, u=2)
+        loaded = {}
+
+        def load(src, tag, k):
+            b, c = divmod(k, PASSES)
+            rows = raw.tile([P, PACK, CHUNK], BF16, tag=tag, name=tag)
+            nc.sync.dma_start(
+                out=rows[:],
+                in_=src[c * K_PASS : (c + 1) * K_PASS, b * CHUNK : (b + 1) * CHUNK].rearrange("(p t) n -> p t n", t=PACK),
+            )
+            loaded[(tag, k)] = rows
+
+        def pieces(j):
+            r, passes = chunks[j]
+            n0, width = RANGES[r]
+            return [((n0 // CHUNK) * PASSES + c, n0 % CHUNK, width, q * width) for q, c in enumerate(passes)]
+
+        def by_runs(rows, lo, width):
+            return rows[:, :, lo : lo + width].rearrange("p t (c i) -> p c t i", i=4)
+
+        def grouped(tile_, lo, width):
+            return tile_[:, lo : lo + width, :].rearrange("p (c i) t -> p c t i", i=4)
+
+        x_sb = {}
+        xg = {}
+        lg = {}
+
+        def x_load(i):
+            x_sb[i] = xin.tile([P, IN], BF16, tag="x_sb", name="x_sb")
+            nc.sync.dma_start(out=x_sb[i][:], in_=input_tensor[i * P : (i + 1) * P, :])
+
+        def x_transpose(i):
+            words = x_sb[i][:].bitcast(F32)
+            xg[i] = xwork.tile([P, PASSES * P * PACK], BF16, tag="xg", name="xg", align_bytes=64)
+            xg_words = xg[i][:].bitcast(F32).rearrange("p (c r u) -> p c r u", c=PASSES, u=2)
             for half in range(PASSES // 2):
-                xt = psum.tile([P, 2, 2, P], F32, tag="xt")
+                pool, tag = ((psa, "s"), (psa, "a"), (psz, "z"))[(2 * i + half) % 3]
+                xt = pool.tile([P, 2, 2, P], F32, tag=tag, name=tag)
                 for c2 in range(2):
                     c = 2 * half + c2
                     for u in range(2):
@@ -61,85 +118,249 @@ def tile_nalu_kernel(tc, input_tensor, W_hat, M_hat, gate, out):
                 nc.vector.tensor_copy(
                     out=xg_words[:, 2 * half : 2 * half + 2], in_=xt[:].rearrange("p c u r -> p c r u")
                 )
-            xa = xin.tile([P, PASSES * P * PACK], BF16)
+
+        def x_quantise(i):
+            nc.vector.quantize_mx(out=x_codes[:, i, :].bitcast(FP8X4), scales=x_scales[:, i, :], in_=xg[i][:])
+
+        def x_abs(i):
             nc.vector.tensor_single_scalar(
-                out=xa[:].bitcast(I32), in_=xg[:].bitcast(I32), scalar=0x7FFF7FFF, op=ALU.bitwise_and
+                out=xg[i][:].bitcast(I32), in_=xg[i][:].bitcast(I32), scalar=0x7FFF7FFF, op=ALU.bitwise_and
             )
-            lg = xin.tile([P, PASSES * P * PACK], BF16, align_bytes=64)
-            nc.scalar.activation(out=lg[:], in_=xa[:], func=ACT.Ln, bias=eps[:], scale=1.0)
-            nc.vector.quantize_mx(out=x_codes[:, i, :].bitcast(FP8X4), scales=x_scales[:, i, :], in_=xg[:])
-            nc.vector.quantize_mx(out=l_codes[:, i, :].bitcast(FP8X4), scales=l_scales[:, i, :], in_=lg[:])
 
-        def load(src, c, n0, tag):
-            rows = raw.tile([P, PACK, RANGE], BF16, tag=tag, name=tag)
+        def x_log(i):
+            lg[i] = lwork.tile([P, PASSES * P * PACK], BF16, tag="lg", name="lg", align_bytes=64)
+            nc.scalar.activation(out=lg[i][:], in_=xg[i][:], func=ACT.Ln, bias=eps[:], scale=1.0)
+
+        def l_quantise(i):
+            nc.vector.quantize_mx(out=l_codes[:, i, :].bitcast(FP8X4), scales=l_scales[:, i, :], in_=lg[i][:])
+
+        t1 = {}
+        t2 = {}
+        gg = {}
+        wg = {}
+        codes = {}
+
+        def tanh_w(j):
+            t1[j] = fac.tile([P, CHUNK, PACK], F32, tag="t1", name="t1")
+            for k, lo, width, pos in pieces(j):
+                nc.scalar.activation(out=grouped(t1[j], pos, width), in_=by_runs(loaded[("wh", k)], lo, width), func=ACT.Tanh)
+
+        def tanh_m(j):
+            t2[j] = fac.tile([P, CHUNK, PACK], F32, tag="t2", name="t2")
+            for k, lo, width, pos in pieces(j):
+                nc.scalar.activation(
+                    out=grouped(t2[j], pos, width), in_=by_runs(loaded[("mh", k)], lo, width), func=ACT.Tanh, scale=0.5
+                )
+
+        def w_product(j):
+            wg[j] = grp.tile([P, CHUNK * PACK], BF16, tag="wg", name="wg", align_bytes=64)
+            nc.vector.scalar_tensor_tensor(
+                out=wg[j][:],
+                in0=t2[j][:].rearrange("p n t -> p (n t)"),
+                scalar=1.0,
+                in1=t1[j][:].rearrange("p n t -> p (n t)"),
+                op0=ALU.add,
+                op1=ALU.mult,
+            )
+
+        def w_quantise(j):
+            wc = wq.tile([P, CHUNK], U32, tag="wc", name="wc", align_bytes=64)
+            ws = wq.tile([P, CHUNK], U8, tag="ws", name="ws", align_bytes=64)
+            nc.vector.quantize_mx(out=wc[:].bitcast(FP8X4), scales=ws[:], in_=wg[j][:])
+            codes[("w", j)] = (wc, ws)
+
+        def g_regroup(j):
+            gg[j] = grp.tile([P, CHUNK, PACK], BF16, tag="gg", name="gg", align_bytes=64)
+            for k, lo, width, pos in pieces(j):
+                nc.vector.tensor_copy(out=grouped(gg[j], pos, width), in_=by_runs(loaded[("gr", k)], lo, width))
+
+        def g_quantise(j):
+            gc = gq.tile([P, CHUNK], U32, tag="gc", name="gc", align_bytes=64)
+            gs = gq.tile([P, CHUNK], U8, tag="gs", name="gs", align_bytes=64)
+            nc.vector.quantize_mx(out=gc[:].bitcast(FP8X4), scales=gs[:], in_=gg[j][:].rearrange("p n t -> p (n t)"))
+            codes[("g", j)] = (gc, gs)
+
+        def product(acc, lhs_codes, lhs_scales, kind, e):
+            r, rows = units[e]
+            width = RANGES[r][1]
+            per = CHUNK // width
+            for q, i in enumerate(rows):
+                for c in range(PASSES):
+                    rc, rs = codes[(kind, first_chunk[r] + c // per)]
+                    lo = (c % per) * width
+                    nc.tensor.matmul_mx(
+                        out=acc[:, q * width : (q + 1) * width],
+                        lhsT=lhs_codes[:, i, c * P : (c + 1) * P].bitcast(FP8X4),
+                        lhsT_scale=lhs_scales[:, i, c * P : (c + 1) * P],
+                        rhs=rc[:, lo : lo + width].bitcast(FP8X4),
+                        rhs_scale=rs[:, lo : lo + width],
+                        start=(c == 0),
+                        stop=(c == PASSES - 1),
+                    )
+
+        z = {}
+        s2 = {}
+        a2 = {}
+        th = {}
+        m = {}
+
+        def pe_gate(e):
+            z[e] = psz.tile([P, CHUNK], F32, tag="z", name="z")
+            product(z[e], x_codes, x_scales, "g", e)
+
+        def pe_w(e):
+            s2[e] = psa.tile([P, CHUNK], F32, tag="s", name="s")
+            product(s2[e], l_codes, l_scales, "w", e)
+            a2[e] = psa.tile([P, CHUNK], F32, tag="a", name="a")
+            product(a2[e], x_codes, x_scales, "w", e)
+
+        def epi_gate(e):
+            th[e] = gates.tile([P, CHUNK], F32, tag="th", name="th")
+            nc.scalar.activation(out=th[e][:], in_=z[e][:], func=ACT.Tanh, scale=0.5)
+
+        def epi_exp(e):
+            m[e] = epi.tile([P, CHUNK], F32, tag="m", name="m")
+            nc.scalar.activation(out=m[e][:], in_=s2[e][:], func=ACT.Exp, scale=0.5)
+
+        def epi_vector(e):
+            r, rows = units[e]
+            n0, width = RANGES[r]
+            d = epi.tile([P, CHUNK], F32, tag="d", name="d")
+            nc.vector.scalar_tensor_tensor(out=d[:], in0=a2[e][:], scalar=0.5, in1=m[e][:], op0=ALU.mult, op1=ALU.subtract)
+            nc.vector.scalar_tensor_tensor(out=d[:], in0=th[e][:], scalar=1.0, in1=d[:], op0=ALU.add, op1=ALU.mult)
+            nc.vector.scalar_tensor_tensor(out=m[e][:], in0=d[:], scalar=0.5, in1=m[e][:], op0=ALU.mult, op1=ALU.add)
             nc.sync.dma_start(
-                out=rows[:],
-                in_=src[c * K_PASS : (c + 1) * K_PASS, n0 : n0 + RANGE].rearrange("(p t) n -> p t n", t=PACK),
+                out=out[rows[0] * P : (rows[-1] + 1) * P, n0 : n0 + width].rearrange("(i p) n -> p i n", p=P),
+                in_=m[e][:].rearrange("p (i n) -> p i n", n=width),
             )
-            return rows
 
-        def by_runs(rows):
-            return rows[:].rearrange("p t (c i) -> p c t i", i=4)
+        n_chunks = len(chunks)
+        n_loads = OUT // CHUNK * PASSES
+        load(W_hat, "wh", 0)
+        x_load(0)
+        load(M_hat, "mh", 0)
+        x_load(1)
+        load(W_hat, "wh", 1)
+        x_load(2)
+        load(M_hat, "mh", 1)
+        x_transpose(0)
+        x_load(3)
+        load(gate, "gr", 0)
+        load(gate, "gr", 1)
+        load(W_hat, "wh", 2)
+        load(M_hat, "mh", 2)
+        load(gate, "gr", 2)
+        load(gate, "gr", 3)
+        load(W_hat, "wh", 3)
+        load(M_hat, "mh", 3)
 
-        def grouped(tile_):
-            return tile_[:].rearrange("p (c i) t -> p c t i", i=4)
+        tanh_w(0)
+        tanh_m(0)
+        tanh_w(1)
+        tanh_m(1)
+        load(W_hat, "wh", 4)
+        load(M_hat, "mh", 4)
+        load(W_hat, "wh", 5)
+        load(M_hat, "mh", 5)
+        x_transpose(1)
+        x_quantise(0)
+        x_abs(0)
+        w_product(0)
+        x_transpose(2)
+        x_quantise(1)
+        x_abs(1)
+        w_quantise(0)
+        x_transpose(3)
+        x_quantise(2)
+        x_abs(2)
+        w_product(1)
+        x_quantise(3)
+        x_abs(3)
+        w_quantise(1)
+        x_log(0)
+        x_log(1)
+        for g in range(4):
+            if g + 2 < ROW_TILES:
+                x_log(g + 2)
+            g_regroup(g)
+            if g > 0:
+                g_quantise(g - 1)
+            l_quantise(g)
+        g_quantise(3)
+        for g in range(4):
+            load(gate, "gr", RAW_BUFS + g)
 
-        def product(acc, lhs_codes, lhs_scales, i, rhs_codes, rhs_scales):
-            for c in range(PASSES):
-                nc.tensor.matmul_mx(
-                    out=acc[:],
-                    lhsT=lhs_codes[:, i, c * P : (c + 1) * P].bitcast(FP8X4),
-                    lhsT_scale=lhs_scales[:, i, c * P : (c + 1) * P],
-                    rhs=rhs_codes[:, c, :].bitcast(FP8X4),
-                    rhs_scale=rhs_scales[:, c, :],
-                    start=(c == 0),
-                    stop=(c == PASSES - 1),
-                )
+        state = {"z": 0, "sa": 0, "th": -1, "ex": -1, "d": -1, "w": 1, "g": 3}
 
-        for n0 in range(0, OUT, RANGE):
-            w_codes = wq.tile([P, PASSES, RANGE], U32, align_bytes=64)
-            w_scales = wq.tile([P, PASSES, RANGE], U8, align_bytes=64)
-            g_codes = wq.tile([P, PASSES, RANGE], U32, align_bytes=64)
-            g_scales = wq.tile([P, PASSES, RANGE], U8, align_bytes=64)
-            for c in range(PASSES):
-                gr = load(gate, c, n0, "gr")
-                gg = grp.tile([P, RANGE, PACK], BF16, align_bytes=64)
-                nc.vector.tensor_copy(out=grouped(gg), in_=by_runs(gr))
-                wh = load(W_hat, c, n0, "wh")
-                mh = load(M_hat, c, n0, "mh")
-                t1 = fac.tile([P, RANGE, PACK], F32)
-                nc.scalar.activation(out=grouped(t1), in_=by_runs(wh), func=ACT.Tanh)
-                t2 = fac.tile([P, RANGE, PACK], F32)
-                nc.scalar.activation(out=grouped(t2), in_=by_runs(mh), func=ACT.Tanh, scale=0.5)
-                nc.vector.quantize_mx(
-                    out=g_codes[:, c, :].bitcast(FP8X4), scales=g_scales[:, c, :], in_=gg[:].rearrange("p n t -> p (n t)")
-                )
-                wg = grp.tile([P, RANGE * PACK], BF16, align_bytes=64)
-                nc.vector.scalar_tensor_tensor(
-                    out=wg[:],
-                    in0=t2[:].rearrange("p n t -> p (n t)"),
-                    scalar=1.0,
-                    in1=t1[:].rearrange("p n t -> p (n t)"),
-                    op0=ALU.add,
-                    op1=ALU.mult,
-                )
-                nc.vector.quantize_mx(out=w_codes[:, c, :].bitcast(FP8X4), scales=w_scales[:, c, :], in_=wg[:])
+        def pe_ready():
+            go = True
+            while go:
+                go = False
+                e = state["sa"]
+                if e < len(units) and last_chunk[units[e][0]] <= state["w"] and e - 3 <= min(state["ex"], state["d"]) and e < state["z"]:
+                    pe_w(e)
+                    state["sa"] = e + 1
+                    go = True
+                e = state["z"]
+                if e < len(units) and last_chunk[units[e][0]] <= state["g"] and e - 2 <= state["th"]:
+                    pe_gate(e)
+                    state["z"] = e + 1
+                    go = True
 
-            for i in range(ROW_TILES):
-                z = psum.tile([P, RANGE], F32, tag="z")
-                product(z, x_codes, x_scales, i, g_codes, g_scales)
-                a2 = psum.tile([P, RANGE], F32, tag="a2")
-                product(a2, x_codes, x_scales, i, w_codes, w_scales)
-                s2 = psum.tile([P, RANGE], F32, tag="s2")
-                product(s2, l_codes, l_scales, i, w_codes, w_scales)
-                th = epi.tile([P, RANGE], F32)
-                nc.scalar.activation(out=th[:], in_=z[:], func=ACT.Tanh, scale=0.5)
-                m = epi.tile([P, RANGE], F32)
-                nc.scalar.activation(out=m[:], in_=s2[:], func=ACT.Exp, scale=0.5)
-                d = epi.tile([P, RANGE], F32)
-                nc.vector.scalar_tensor_tensor(out=d[:], in0=a2[:], scalar=0.5, in1=m[:], op0=ALU.mult, op1=ALU.subtract)
-                e = epi.tile([P, RANGE], F32)
-                nc.vector.scalar_tensor_tensor(out=e[:], in0=th[:], scalar=1.0, in1=d[:], op0=ALU.add, op1=ALU.mult)
-                o = epi.tile([P, RANGE], F32)
-                nc.vector.scalar_tensor_tensor(out=o[:], in0=e[:], scalar=0.5, in1=m[:], op0=ALU.mult, op1=ALU.add)
-                nc.sync.dma_start(out=out[i * P : (i + 1) * P, n0 : n0 + RANGE], in_=o[:])
+        def gate_tanh(e):
+            epi_gate(e)
+            state["th"] = e
+            pe_ready()
+
+        def exp(e):
+            epi_exp(e)
+            state["ex"] = e
+
+        def blend(e):
+            epi_vector(e)
+            state["d"] = e
+            pe_ready()
+
+        pe_ready()
+        for j in range(2, n_chunks):
+            tanh_w(j)
+            for e in TH_AFTER_W.get(j, ()):
+                gate_tanh(e)
+            for e in EX_AFTER_W.get(j, ()):
+                exp(e)
+            tanh_m(j)
+            if j + RAW_BUFS < n_loads:
+                load(W_hat, "wh", j + RAW_BUFS)
+                load(M_hat, "mh", j + RAW_BUFS)
+            for e in TH_AFTER_M.get(j, ()):
+                gate_tanh(e)
+            state["w"] = j - 1
+            pe_ready()
+            for e in EX_AFTER_M.get(j, ()):
+                exp(e)
+            for e in EX_AFTER_W.get(j, ()):
+                blend(e)
+            w_product(j)
+            todo = GATE_SLOTS.get(j, ())
+            for g in todo[:1]:
+                g_regroup(g)
+            w_quantise(j)
+            for g in todo[1:]:
+                g_regroup(g)
+            for g in todo[:1]:
+                g_quantise(g)
+                state["g"] = g
+            for e in EX_AFTER_M.get(j, ()):
+                blend(e)
+            for g in todo[1:]:
+                g_quantise(g)
+                state["g"] = g
+            pe_ready()
+            for g in todo:
+                if g + RAW_BUFS < n_loads:
+                    load(gate, "gr", g + RAW_BUFS)
+        state["w"] = n_chunks - 1
+        pe_ready()
+        for e in range(state["d"] + 1, len(units)):
+            exp(e)
+            blend(e)

@@ -18,51 +18,51 @@ K_PASS = P * PACK
 B, IN, OUT = 512, 2048, 1536
 PASSES = IN // K_PASS
 ROW_TILES = B // P
-CHUNK = 512
+BLOCK = 512
 EPS = 1e-07
 FLOPS = 3 * 2 * B * IN * OUT
 
-RANGES = ((0, 512), (512, 512), (1024, 256), (1280, 128), (1408, 128))
-RAW_BUFS = 4
-PINNED = True
+WIDE = tuple(((c, b * BLOCK, BLOCK),) for b in range(2) for c in range(PASSES))
+W_CHUNKS = WIDE + (
+    ((0, 1024, 256), (1, 1024, 256)),
+    ((2, 1024, 256), (3, 1024, 256)),
+    ((0, 1280, 128), (1, 1280, 128), (2, 1280, 128), (3, 1280, 128)),
+    ((0, 1408, 128), (1, 1408, 128)),
+    ((2, 1408, 128), (3, 1408, 128)),
+)
+G_CHUNKS = WIDE + (
+    ((0, 1024, 256), (1, 1024, 256)),
+    ((2, 1024, 256), (3, 1024, 256)),
+    ((0, 1280, 128), (1, 1280, 128), (2, 1280, 128), (3, 1280, 128)),
+    ((0, 1408, 128), (1, 1408, 128), (2, 1408, 128), (3, 1408, 128)),
+)
+UNITS = (
+    tuple((0, 512, (i,), 3, 3) for i in range(ROW_TILES))
+    + tuple((512, 512, (i,), 7, 7) for i in range(ROW_TILES))
+    + ((1024, 256, (0, 1), 9, 9), (1024, 256, (2, 3), 9, 9))
+    + ((1280, 128, (0, 1, 2, 3), 10, 10), (1408, 128, (0, 1, 2, 3), 12, 11))
+)
+RAW_BUFS = 5
 GATE_SLOTS = {2: (4, 5), 3: (6,), 4: (7, 8), 5: (9,), 6: (10,), 7: (11,)}
 TH_AFTER_W = {3: (0,), 4: (2,), 7: (4,), 8: (6,), 9: (8,)}
-TH_AFTER_M = {3: (1,), 4: (3,), 7: (5,), 8: (7,), 9: (9,), 11: (10, 11)}
+TH_AFTER_M = {3: (1,), 4: (3,), 7: (5,), 8: (7,), 9: (9,), 12: (10, 11)}
 EX_AFTER_W = {5: (0,), 6: (2,), 9: (4,), 10: (6,), 11: (8,)}
-EX_AFTER_M = {5: (1,), 6: (3,), 9: (5,), 10: (7,), 11: (9,)}
+EX_AFTER_M = {5: (1,), 6: (3,), 9: (5,), 10: (7,), 12: (9, 10)}
 
 
 def tile_nalu_kernel(tc, input_tensor, W_hat, M_hat, gate, out):
     nc = tc.nc
-    chunks = []
-    units = []
-    last_chunk = []
-    for r, (n0, width) in enumerate(RANGES):
-        per = CHUNK // width
-        for c0 in range(0, PASSES, per):
-            chunks.append((r, tuple(range(c0, c0 + per))))
-        last_chunk.append(len(chunks) - 1)
-        for i0 in range(0, ROW_TILES, per):
-            units.append((r, tuple(range(i0, i0 + per))))
-    first_chunk = [last_chunk[r] + 1 - PASSES * RANGES[r][1] // CHUNK for r in range(len(RANGES))]
-
     with ExitStack() as ctx:
         const = ctx.enter_context(tc.tile_pool(name="const", bufs=1))
         keep = ctx.enter_context(tc.tile_pool(name="keep", bufs=1))
-        xin = ctx.enter_context(tc.tile_pool(name="xin", bufs=3))
-        xwork = ctx.enter_context(tc.tile_pool(name="xwork", bufs=4))
-        lwork = ctx.enter_context(tc.tile_pool(name="lwork", bufs=4))
         raw = ctx.enter_context(tc.tile_pool(name="raw", bufs=RAW_BUFS))
-        fac = ctx.enter_context(tc.tile_pool(name="fac", bufs=2))
+        fac = ctx.enter_context(tc.tile_pool(name="fac", bufs=3))
         grp = ctx.enter_context(tc.tile_pool(name="grp", bufs=2))
-        wq = ctx.enter_context(tc.tile_pool(name="wq", bufs=9))
-        gq = ctx.enter_context(tc.tile_pool(name="gq", bufs=8))
-        epi = ctx.enter_context(tc.tile_pool(name="epi", bufs=3))
-        gates = ctx.enter_context(tc.tile_pool(name="gates", bufs=6))
+        wq = ctx.enter_context(tc.tile_pool(name="wq", bufs=8))
+        gq = ctx.enter_context(tc.tile_pool(name="gq", bufs=7))
         psz = ctx.enter_context(tc.psum_pool(name="psz", bufs=2))
         psa = ctx.enter_context(tc.psum_pool(name="psa", bufs=3))
-        if PINNED:
-            ctx.enter_context(tc.manual_schedule())
+        ctx.enter_context(tc.manual_schedule())
 
         ident = const.tile([P, P], F32)
         make_identity(nc, ident[:])
@@ -78,82 +78,46 @@ def tile_nalu_kernel(tc, input_tensor, W_hat, M_hat, gate, out):
 
         def load(src, tag, k):
             b, c = divmod(k, PASSES)
-            rows = raw.tile([P, PACK, CHUNK], BF16, tag=tag, name=tag)
+            rows = raw.tile([P, PACK, BLOCK], BF16, tag=tag, name=tag)
             nc.sync.dma_start(
                 out=rows[:],
-                in_=src[c * K_PASS : (c + 1) * K_PASS, b * CHUNK : (b + 1) * CHUNK].rearrange("(p t) n -> p t n", t=PACK),
+                in_=src[c * K_PASS : (c + 1) * K_PASS, b * BLOCK : (b + 1) * BLOCK].rearrange("(p t) n -> p t n", t=PACK),
             )
             loaded[(tag, k)] = rows
 
-        def pieces(j):
-            r, passes = chunks[j]
-            n0, width = RANGES[r]
-            return [((n0 // CHUNK) * PASSES + c, n0 % CHUNK, width, q * width) for q, c in enumerate(passes)]
-
-        def by_runs(rows, lo, width):
-            return rows[:, :, lo : lo + width].rearrange("p t (c i) -> p c t i", i=4)
+        def by_runs(tag, piece):
+            c, n0, width = piece
+            rows = loaded[(tag, n0 // BLOCK * PASSES + c)]
+            return rows[:, :, n0 % BLOCK : n0 % BLOCK + width].rearrange("p t (c i) -> p c t i", i=4)
 
         def grouped(tile_, lo, width):
             return tile_[:, lo : lo + width, :].rearrange("p (c i) t -> p c t i", i=4)
 
-        x_sb = {}
-        xg = {}
-        lg = {}
-
-        def x_load(i):
-            x_sb[i] = xin.tile([P, IN], BF16, tag="x_sb", name="x_sb")
-            nc.sync.dma_start(out=x_sb[i][:], in_=input_tensor[i * P : (i + 1) * P, :])
-
-        def x_transpose(i):
-            words = x_sb[i][:].bitcast(F32)
-            xg[i] = xwork.tile([P, PASSES * P * PACK], BF16, tag="xg", name="xg", align_bytes=64)
-            xg_words = xg[i][:].bitcast(F32).rearrange("p (c r u) -> p c r u", c=PASSES, u=2)
-            for half in range(PASSES // 2):
-                pool, tag = ((psa, "s"), (psa, "a"), (psz, "z"))[(2 * i + half) % 3]
-                xt = pool.tile([P, 2, 2, P], F32, tag=tag, name=tag)
-                for c2 in range(2):
-                    c = 2 * half + c2
-                    for u in range(2):
-                        nc.tensor.transpose(xt[:, c2, u, :], words[:, 256 * c + u : 256 * (c + 1) : 2], ident[:])
-                nc.vector.tensor_copy(
-                    out=xg_words[:, 2 * half : 2 * half + 2], in_=xt[:].rearrange("p c u r -> p c r u")
-                )
-
-        def x_quantise(i):
-            nc.vector.quantize_mx(out=x_codes[:, i, :].bitcast(FP8X4), scales=x_scales[:, i, :], in_=xg[i][:])
-
-        def x_abs(i):
-            nc.vector.tensor_single_scalar(
-                out=xg[i][:].bitcast(I32), in_=xg[i][:].bitcast(I32), scalar=0x7FFF7FFF, op=ALU.bitwise_and
-            )
-
-        def x_log(i):
-            lg[i] = lwork.tile([P, PASSES * P * PACK], BF16, tag="lg", name="lg", align_bytes=64)
-            nc.scalar.activation(out=lg[i][:], in_=xg[i][:], func=ACT.Ln, bias=eps[:], scale=1.0)
-
-        def l_quantise(i):
-            nc.vector.quantize_mx(out=l_codes[:, i, :].bitcast(FP8X4), scales=l_scales[:, i, :], in_=lg[i][:])
+        def words(chunk):
+            return sum(width for c, n0, width in chunk)
 
         t1 = {}
         t2 = {}
         gg = {}
         wg = {}
-        codes = {}
+        where = {}
+
+        def tanh_pass(j, tag, scale):
+            res = fac.tile([P, words(W_CHUNKS[j]), PACK], F32, tag="t" + tag, name="t" + tag)
+            lo = 0
+            for piece in W_CHUNKS[j]:
+                nc.scalar.activation(out=grouped(res, lo, piece[2]), in_=by_runs(tag, piece), func=ACT.Tanh, scale=scale)
+                lo += piece[2]
+            return res
 
         def tanh_w(j):
-            t1[j] = fac.tile([P, CHUNK, PACK], F32, tag="t1", name="t1")
-            for k, lo, width, pos in pieces(j):
-                nc.scalar.activation(out=grouped(t1[j], pos, width), in_=by_runs(loaded[("wh", k)], lo, width), func=ACT.Tanh)
+            t1[j] = tanh_pass(j, "wh", 1.0)
 
         def tanh_m(j):
-            t2[j] = fac.tile([P, CHUNK, PACK], F32, tag="t2", name="t2")
-            for k, lo, width, pos in pieces(j):
-                nc.scalar.activation(
-                    out=grouped(t2[j], pos, width), in_=by_runs(loaded[("mh", k)], lo, width), func=ACT.Tanh, scale=0.5
-                )
+            t2[j] = tanh_pass(j, "mh", 0.5)
 
         def w_product(j):
-            wg[j] = grp.tile([P, CHUNK * PACK], BF16, tag="wg", name="wg", align_bytes=64)
+            wg[j] = grp.tile([P, words(W_CHUNKS[j]) * PACK], BF16, tag="wg", name="wg", align_bytes=64)
             nc.vector.scalar_tensor_tensor(
                 out=wg[j][:],
                 in0=t2[j][:].rearrange("p n t -> p (n t)"),
@@ -163,37 +127,41 @@ def tile_nalu_kernel(tc, input_tensor, W_hat, M_hat, gate, out):
                 op1=ALU.mult,
             )
 
+        def quantise(kind, pool, chunk, values):
+            n = words(chunk)
+            cod = pool.tile([P, n], U32, tag=kind + "c", name=kind + "c", align_bytes=64)
+            sca = pool.tile([P, n], U8, tag=kind + "s", name=kind + "s", align_bytes=64)
+            nc.vector.quantize_mx(out=cod[:].bitcast(FP8X4), scales=sca[:], in_=values)
+            lo = 0
+            for c, n0, width in chunk:
+                for off in range(0, width, P):
+                    where[(kind, c, n0 + off)] = (cod, sca, lo + off)
+                lo += width
+
         def w_quantise(j):
-            wc = wq.tile([P, CHUNK], U32, tag="wc", name="wc", align_bytes=64)
-            ws = wq.tile([P, CHUNK], U8, tag="ws", name="ws", align_bytes=64)
-            nc.vector.quantize_mx(out=wc[:].bitcast(FP8X4), scales=ws[:], in_=wg[j][:])
-            codes[("w", j)] = (wc, ws)
+            quantise("w", wq, W_CHUNKS[j], wg[j][:])
 
         def g_regroup(j):
-            gg[j] = grp.tile([P, CHUNK, PACK], BF16, tag="gg", name="gg", align_bytes=64)
-            for k, lo, width, pos in pieces(j):
-                nc.vector.tensor_copy(out=grouped(gg[j], pos, width), in_=by_runs(loaded[("gr", k)], lo, width))
+            gg[j] = grp.tile([P, BLOCK, PACK], BF16, tag="gg", name="gg", align_bytes=64)
+            lo = 0
+            for piece in G_CHUNKS[j]:
+                nc.vector.tensor_copy(out=grouped(gg[j], lo, piece[2]), in_=by_runs("gr", piece))
+                lo += piece[2]
 
         def g_quantise(j):
-            gc = gq.tile([P, CHUNK], U32, tag="gc", name="gc", align_bytes=64)
-            gs = gq.tile([P, CHUNK], U8, tag="gs", name="gs", align_bytes=64)
-            nc.vector.quantize_mx(out=gc[:].bitcast(FP8X4), scales=gs[:], in_=gg[j][:].rearrange("p n t -> p (n t)"))
-            codes[("g", j)] = (gc, gs)
+            quantise("g", gq, G_CHUNKS[j], gg[j][:].rearrange("p n t -> p (n t)"))
 
         def product(acc, lhs_codes, lhs_scales, kind, e):
-            r, rows = units[e]
-            width = RANGES[r][1]
-            per = CHUNK // width
+            n0, width, rows = UNITS[e][:3]
             for q, i in enumerate(rows):
                 for c in range(PASSES):
-                    rc, rs = codes[(kind, first_chunk[r] + c // per)]
-                    lo = (c % per) * width
+                    cod, sca, lo = where[(kind, c, n0)]
                     nc.tensor.matmul_mx(
                         out=acc[:, q * width : (q + 1) * width],
                         lhsT=lhs_codes[:, i, c * P : (c + 1) * P].bitcast(FP8X4),
                         lhsT_scale=lhs_scales[:, i, c * P : (c + 1) * P],
-                        rhs=rc[:, lo : lo + width].bitcast(FP8X4),
-                        rhs_scale=rs[:, lo : lo + width],
+                        rhs=cod[:, lo : lo + width].bitcast(FP8X4),
+                        rhs_scale=sca[:, lo : lo + width],
                         start=(c == 0),
                         stop=(c == PASSES - 1),
                     )
@@ -201,128 +169,173 @@ def tile_nalu_kernel(tc, input_tensor, W_hat, M_hat, gate, out):
         z = {}
         s2 = {}
         a2 = {}
-        th = {}
-        m = {}
-
-        def pe_gate(e):
-            z[e] = psz.tile([P, CHUNK], F32, tag="z", name="z")
-            product(z[e], x_codes, x_scales, "g", e)
-
-        def pe_w(e):
-            s2[e] = psa.tile([P, CHUNK], F32, tag="s", name="s")
-            product(s2[e], l_codes, l_scales, "w", e)
-            a2[e] = psa.tile([P, CHUNK], F32, tag="a", name="a")
-            product(a2[e], x_codes, x_scales, "w", e)
-
-        def epi_gate(e):
-            th[e] = gates.tile([P, CHUNK], F32, tag="th", name="th")
-            nc.scalar.activation(out=th[e][:], in_=z[e][:], func=ACT.Tanh, scale=0.5)
-
-        def epi_exp(e):
-            m[e] = epi.tile([P, CHUNK], F32, tag="m", name="m")
-            nc.scalar.activation(out=m[e][:], in_=s2[e][:], func=ACT.Exp, scale=0.5)
-
-        def epi_vector(e):
-            r, rows = units[e]
-            n0, width = RANGES[r]
-            d = epi.tile([P, CHUNK], F32, tag="d", name="d")
-            nc.vector.scalar_tensor_tensor(out=d[:], in0=a2[e][:], scalar=0.5, in1=m[e][:], op0=ALU.mult, op1=ALU.subtract)
-            nc.vector.scalar_tensor_tensor(out=d[:], in0=th[e][:], scalar=1.0, in1=d[:], op0=ALU.add, op1=ALU.mult)
-            nc.vector.scalar_tensor_tensor(out=m[e][:], in0=d[:], scalar=0.5, in1=m[e][:], op0=ALU.mult, op1=ALU.add)
-            nc.sync.dma_start(
-                out=out[rows[0] * P : (rows[-1] + 1) * P, n0 : n0 + width].rearrange("(i p) n -> p i n", p=P),
-                in_=m[e][:].rearrange("p (i n) -> p i n", n=width),
-            )
-
-        n_chunks = len(chunks)
-        n_loads = OUT // CHUNK * PASSES
-        load(W_hat, "wh", 0)
-        x_load(0)
-        load(M_hat, "mh", 0)
-        x_load(1)
-        load(W_hat, "wh", 1)
-        x_load(2)
-        load(M_hat, "mh", 1)
-        x_transpose(0)
-        x_load(3)
-        load(gate, "gr", 0)
-        load(gate, "gr", 1)
-        load(W_hat, "wh", 2)
-        load(M_hat, "mh", 2)
-        load(gate, "gr", 2)
-        load(gate, "gr", 3)
-        load(W_hat, "wh", 3)
-        load(M_hat, "mh", 3)
-
-        tanh_w(0)
-        tanh_m(0)
-        tanh_w(1)
-        tanh_m(1)
-        load(W_hat, "wh", 4)
-        load(M_hat, "mh", 4)
-        load(W_hat, "wh", 5)
-        load(M_hat, "mh", 5)
-        x_transpose(1)
-        x_quantise(0)
-        x_abs(0)
-        w_product(0)
-        x_transpose(2)
-        x_quantise(1)
-        x_abs(1)
-        w_quantise(0)
-        x_transpose(3)
-        x_quantise(2)
-        x_abs(2)
-        w_product(1)
-        x_quantise(3)
-        x_abs(3)
-        w_quantise(1)
-        x_log(0)
-        x_log(1)
-        for g in range(4):
-            if g + 2 < ROW_TILES:
-                x_log(g + 2)
-            g_regroup(g)
-            if g > 0:
-                g_quantise(g - 1)
-            l_quantise(g)
-        g_quantise(3)
-        for g in range(4):
-            load(gate, "gr", RAW_BUFS + g)
-
-        state = {"z": 0, "sa": 0, "th": -1, "ex": -1, "d": -1, "w": 1, "g": 3}
+        state = {"z": 0, "sa": 0, "th": -1, "ex": -1, "d": -1, "w": -1, "g": -1}
 
         def pe_ready():
             go = True
             while go:
                 go = False
                 e = state["sa"]
-                if e < len(units) and last_chunk[units[e][0]] <= state["w"] and e - 3 <= min(state["ex"], state["d"]) and e < state["z"]:
-                    pe_w(e)
+                if e < min(len(UNITS), state["z"]) and UNITS[e][3] <= state["w"] and e - 3 <= min(state["ex"], state["d"]):
+                    s2[e] = psa.tile([P, BLOCK], F32, tag="s", name="s")
+                    product(s2[e], l_codes, l_scales, "w", e)
+                    a2[e] = psa.tile([P, BLOCK], F32, tag="a", name="a")
+                    product(a2[e], x_codes, x_scales, "w", e)
                     state["sa"] = e + 1
                     go = True
                 e = state["z"]
-                if e < len(units) and last_chunk[units[e][0]] <= state["g"] and e - 2 <= state["th"]:
-                    pe_gate(e)
+                if e < len(UNITS) and UNITS[e][4] <= state["g"] and e - 2 <= state["th"]:
+                    z[e] = psz.tile([P, BLOCK], F32, tag="z", name="z")
+                    product(z[e], x_codes, x_scales, "g", e)
                     state["z"] = e + 1
                     go = True
 
+        with tc.tile_pool(name="xin", bufs=3) as xin, tc.tile_pool(name="xwork", bufs=4) as xwork:
+            x_sb = {}
+            xg = {}
+            lg = {}
+
+            def x_load(i):
+                x_sb[i] = xin.tile([P, IN], BF16, tag="x_sb", name="x_sb")
+                nc.sync.dma_start(out=x_sb[i][:], in_=input_tensor[i * P : (i + 1) * P, :])
+
+            def x_transpose(i):
+                pairs = x_sb[i][:].bitcast(F32)
+                xg[i] = xwork.tile([P, PASSES * P * PACK], BF16, tag="xg", name="xg", align_bytes=64)
+                xg_pairs = xg[i][:].bitcast(F32).rearrange("p (c r u) -> p c r u", c=PASSES, u=2)
+                for half in range(PASSES // 2):
+                    pool, tag = ((psa, "s"), (psa, "a"), (psz, "z"))[(2 * i + half) % 3]
+                    xt = pool.tile([P, 2, 2, P], F32, tag=tag, name=tag)
+                    for c2 in range(2):
+                        c = 2 * half + c2
+                        for u in range(2):
+                            nc.tensor.transpose(xt[:, c2, u, :], pairs[:, 256 * c + u : 256 * (c + 1) : 2], ident[:])
+                    nc.vector.tensor_copy(
+                        out=xg_pairs[:, 2 * half : 2 * half + 2], in_=xt[:].rearrange("p c u r -> p c r u")
+                    )
+
+            def x_quantise(i):
+                nc.vector.quantize_mx(out=x_codes[:, i, :].bitcast(FP8X4), scales=x_scales[:, i, :], in_=xg[i][:])
+
+            def x_abs(i):
+                nc.vector.tensor_single_scalar(
+                    out=xg[i][:].bitcast(I32), in_=xg[i][:].bitcast(I32), scalar=0x7FFF7FFF, op=ALU.bitwise_and
+                )
+
+            def x_log(i):
+                lg[i] = xwork.tile([P, PASSES * P * PACK], BF16, tag="lg", name="lg", align_bytes=64)
+                nc.scalar.activation(out=lg[i][:], in_=xg[i][:], func=ACT.Ln, bias=eps[:], scale=1.0)
+
+            def l_quantise(i):
+                nc.vector.quantize_mx(out=l_codes[:, i, :].bitcast(FP8X4), scales=l_scales[:, i, :], in_=lg[i][:])
+
+            load(W_hat, "wh", 0)
+            x_load(0)
+            load(M_hat, "mh", 0)
+            x_load(1)
+            load(W_hat, "wh", 1)
+            x_load(2)
+            load(M_hat, "mh", 1)
+            x_transpose(0)
+            x_load(3)
+            load(gate, "gr", 0)
+            load(gate, "gr", 1)
+            load(W_hat, "wh", 2)
+            load(M_hat, "mh", 2)
+            load(gate, "gr", 2)
+            load(gate, "gr", 3)
+            for k in range(3, RAW_BUFS):
+                load(W_hat, "wh", k)
+                load(M_hat, "mh", k)
+            load(gate, "gr", 4)
+
+            tanh_w(0)
+            tanh_m(0)
+            tanh_w(1)
+            tanh_m(1)
+            load(W_hat, "wh", RAW_BUFS)
+            load(M_hat, "mh", RAW_BUFS)
+            load(W_hat, "wh", RAW_BUFS + 1)
+            load(M_hat, "mh", RAW_BUFS + 1)
+            x_transpose(1)
+            x_quantise(0)
+            x_abs(0)
+            w_product(0)
+            x_transpose(2)
+            x_quantise(1)
+            x_abs(1)
+            w_quantise(0)
+            x_transpose(3)
+            x_quantise(2)
+            x_abs(2)
+            w_product(1)
+            x_quantise(3)
+            x_abs(3)
+            w_quantise(1)
+            for i in range(ROW_TILES):
+                x_log(i)
+            for g in range(4):
+                g_regroup(g)
+                if g > 0:
+                    g_quantise(g - 1)
+                l_quantise(g)
+            g_quantise(3)
+            for g in range(4):
+                load(gate, "gr", RAW_BUFS + g)
+        state["w"] = 1
+        state["g"] = 3
+
+        epi = ctx.enter_context(tc.tile_pool(name="epi", bufs=3))
+        outs = ctx.enter_context(tc.tile_pool(name="outs", bufs=5))
+        gates = ctx.enter_context(tc.tile_pool(name="gates", bufs=6))
+        th = {}
+        m = {}
+        d = {}
+
         def gate_tanh(e):
-            epi_gate(e)
+            th[e] = gates.tile([P, BLOCK], F32, tag="th", name="th")
+            nc.scalar.activation(out=th[e][:], in_=z[e][:], func=ACT.Tanh, scale=0.5)
             state["th"] = e
             pe_ready()
 
         def exp(e):
-            epi_exp(e)
+            m[e] = outs.tile([P, BLOCK], F32, tag="m", name="m")
+            nc.scalar.activation(out=m[e][:], in_=s2[e][:], func=ACT.Exp, scale=0.5)
             state["ex"] = e
 
-        def blend(e):
-            epi_vector(e)
+        def blend_d(e):
+            d[e] = epi.tile([P, BLOCK], F32, tag="d", name="d")
+            nc.vector.scalar_tensor_tensor(
+                out=d[e][:], in0=a2[e][:], scalar=0.5, in1=m[e][:], op0=ALU.mult, op1=ALU.subtract
+            )
             state["d"] = e
             pe_ready()
 
+        def blend_e(e):
+            nc.vector.scalar_tensor_tensor(out=d[e][:], in0=th[e][:], scalar=1.0, in1=d[e][:], op0=ALU.add, op1=ALU.mult)
+
+        def blend_o(e):
+            n0, width, rows = UNITS[e][:3]
+            nc.vector.scalar_tensor_tensor(out=m[e][:], in0=d[e][:], scalar=0.5, in1=m[e][:], op0=ALU.mult, op1=ALU.add)
+            nc.sync.dma_start(
+                out=out[rows[0] * P : (rows[-1] + 1) * P, n0 : n0 + width].rearrange("(i p) n -> p i n", p=P),
+                in_=m[e][:].rearrange("p (i n) -> p i n", n=width),
+            )
+
+        def g_done(g):
+            g_quantise(g)
+            state["g"] = g
+            pe_ready()
+
+        def in_turn(chains):
+            for step in range(max(len(chain) for chain in chains)):
+                for chain in chains:
+                    if step < len(chain):
+                        chain[step][0](chain[step][1])
+
+        n_loads = OUT // BLOCK * PASSES
         pe_ready()
-        for j in range(2, n_chunks):
+        for j in range(2, len(W_CHUNKS)):
             tanh_w(j)
             for e in TH_AFTER_W.get(j, ()):
                 gate_tanh(e)
@@ -338,29 +351,16 @@ def tile_nalu_kernel(tc, input_tensor, W_hat, M_hat, gate, out):
             pe_ready()
             for e in EX_AFTER_M.get(j, ()):
                 exp(e)
-            for e in EX_AFTER_W.get(j, ()):
-                blend(e)
-            w_product(j)
-            todo = GATE_SLOTS.get(j, ())
-            for g in todo[:1]:
-                g_regroup(g)
-            w_quantise(j)
-            for g in todo[1:]:
-                g_regroup(g)
-            for g in todo[:1]:
-                g_quantise(g)
-                state["g"] = g
-            for e in EX_AFTER_M.get(j, ()):
-                blend(e)
-            for g in todo[1:]:
-                g_quantise(g)
-                state["g"] = g
-            pe_ready()
-            for g in todo:
+            chains = [[(blend_d, e), (blend_e, e), (blend_o, e)] for e in EX_AFTER_W.get(j, ())]
+            chains.append([(w_product, j), (w_quantise, j)])
+            chains.extend([[(g_regroup, g), (g_done, g)] for g in GATE_SLOTS.get(j, ())])
+            chains.extend([[(blend_d, e), (blend_e, e), (blend_o, e)] for e in EX_AFTER_M.get(j, ())])
+            in_turn(chains)
+            for g in GATE_SLOTS.get(j, ()):
                 if g + RAW_BUFS < n_loads:
                     load(gate, "gr", g + RAW_BUFS)
-        state["w"] = n_chunks - 1
+        state["w"] = len(W_CHUNKS) - 1
         pe_ready()
-        for e in range(state["d"] + 1, len(units)):
+        for e in range(state["ex"] + 1, len(UNITS)):
             exp(e)
-            blend(e)
+            in_turn([[(blend_d, e), (blend_e, e), (blend_o, e)]])

@@ -90,6 +90,11 @@ def tile_nalu_kernel(tc, input_tensor, W_hat, M_hat, gate, out):
             rows = loaded[(tag, n0 // BLOCK * PASSES + c)]
             return rows[:, :, n0 % BLOCK : n0 % BLOCK + width].rearrange("p t (c i) -> p c t i", i=4)
 
+        def by_columns(tag, piece):
+            c, n0, width = piece
+            rows = loaded[(tag, n0 // BLOCK * PASSES + c)]
+            return rows[:, :, n0 % BLOCK : n0 % BLOCK + width].rearrange("p t n -> p n t")
+
         def grouped(tile_, lo, width):
             return tile_[:, lo : lo + width, :].rearrange("p (c i) t -> p c t i", i=4)
 
@@ -106,7 +111,7 @@ def tile_nalu_kernel(tc, input_tensor, W_hat, M_hat, gate, out):
             res = fac.tile([P, words(W_CHUNKS[j]), PACK], F32, tag="t" + tag, name="t" + tag)
             lo = 0
             for piece in W_CHUNKS[j]:
-                nc.scalar.activation(out=grouped(res, lo, piece[2]), in_=by_runs(tag, piece), func=ACT.Tanh, scale=scale)
+                nc.scalar.activation(out=res[:, lo : lo + piece[2], :], in_=by_columns(tag, piece), func=ACT.Tanh, scale=scale)
                 lo += piece[2]
             return res
 

@@ -43,11 +43,12 @@ UNITS = (
     + ((1280, 128, (0, 1, 2, 3), 10, 10), (1408, 128, (0, 1, 2, 3), 12, 11))
 )
 RAW_BUFS = 5
-GATE_SLOTS = {2: (4, 5), 3: (6,), 4: (7, 8), 5: (9,), 6: (10,), 7: (11,)}
-TH_AFTER_W = {3: (0,), 4: (2,), 7: (4,), 8: (6,), 9: (8,)}
-TH_AFTER_M = {3: (1,), 4: (3,), 7: (5,), 8: (7,), 9: (9,), 12: (10, 11)}
-EX_AFTER_W = {5: (0,), 6: (2,), 9: (4,), 10: (6,), 11: (8,)}
-EX_AFTER_M = {5: (1,), 6: (3,), 9: (5,), 10: (7,), 12: (9, 10)}
+NATURAL = (2,)
+GATE_SLOTS = {2: (4, 5), 3: (6,), 4: (7, 8), 5: (9,), 7: (10,), 8: (11,)}
+TH_AFTER_W = {3: (0,), 4: (2,), 7: (4,), 8: (6,), 9: (8,), 12: (10,)}
+TH_AFTER_M = {3: (1,), 4: (3,), 7: (5,), 8: (7,), 9: (9,), 12: (11,)}
+EX_AFTER_W = {5: (0,), 6: (1, 2), 7: (3,), 9: (4,), 11: (8,)}
+EX_AFTER_M = {9: (5, 6), 10: (7,), 12: (9, 10)}
 
 
 def tile_nalu_kernel(tc, input_tensor, W_hat, M_hat, gate, out):
@@ -105,9 +106,21 @@ def tile_nalu_kernel(tc, input_tensor, W_hat, M_hat, gate, out):
         t2 = {}
         gg = {}
         wg = {}
+        wn = {}
+        flats = []
         where = {}
 
         def tanh_pass(j, tag, scale):
+            if j in NATURAL:
+                flat = fac.tile([P, PACK, words(W_CHUNKS[j])], F32, tag="t" + tag, name="t" + tag)
+                lo = 0
+                for c, n0, width in W_CHUNKS[j]:
+                    rows = loaded[(tag, n0 // BLOCK * PASSES + c)]
+                    nc.scalar.activation(
+                        out=flat[:, :, lo : lo + width], in_=rows[:, :, n0 % BLOCK : n0 % BLOCK + width], func=ACT.Tanh, scale=scale
+                    )
+                    lo += width
+                return flat
             res = fac.tile([P, words(W_CHUNKS[j]), PACK], F32, tag="t" + tag, name="t" + tag)
             lo = 0
             for piece in W_CHUNKS[j]:
@@ -122,15 +135,27 @@ def tile_nalu_kernel(tc, input_tensor, W_hat, M_hat, gate, out):
             t2[j] = tanh_pass(j, "mh", 0.5)
 
         def w_product(j):
-            wg[j] = grp.tile([P, words(W_CHUNKS[j]) * PACK], BF16, tag="wg", name="wg", align_bytes=64)
+            n = words(W_CHUNKS[j])
+            if j in NATURAL:
+                wn[j] = flats[0].tile([P, PACK, n], BF16, tag="wn", name="wn")
+                res = wn[j][:].rearrange("p t n -> p (t n)")
+            else:
+                wg[j] = grp.tile([P, n * PACK], BF16, tag="wg", name="wg", align_bytes=64)
+                res = wg[j][:]
             nc.vector.scalar_tensor_tensor(
-                out=wg[j][:],
-                in0=t2[j][:].rearrange("p n t -> p (n t)"),
+                out=res,
+                in0=t2[j][:].rearrange("p a b -> p (a b)"),
                 scalar=1.0,
-                in1=t1[j][:].rearrange("p n t -> p (n t)"),
+                in1=t1[j][:].rearrange("p a b -> p (a b)"),
                 op0=ALU.add,
                 op1=ALU.mult,
             )
+
+        def w_regroup(j):
+            n = words(W_CHUNKS[j])
+            wide = grp.tile([P, n, PACK], BF16, tag="wg", name="wg", align_bytes=64)
+            nc.vector.tensor_copy(out=grouped(wide, 0, n), in_=wn[j][:].rearrange("p t (c i) -> p c t i", i=4))
+            wg[j] = wide[:].rearrange("p n t -> p (n t)")
 
         def quantise(kind, pool, chunk, values):
             n = words(chunk)
@@ -293,6 +318,7 @@ def tile_nalu_kernel(tc, input_tensor, W_hat, M_hat, gate, out):
         epi = ctx.enter_context(tc.tile_pool(name="epi", bufs=3))
         outs = ctx.enter_context(tc.tile_pool(name="outs", bufs=5))
         gates = ctx.enter_context(tc.tile_pool(name="gates", bufs=6))
+        flats.append(ctx.enter_context(tc.tile_pool(name="flat", bufs=2)))
         th = {}
         m = {}
         d = {}
@@ -357,7 +383,7 @@ def tile_nalu_kernel(tc, input_tensor, W_hat, M_hat, gate, out):
             for e in EX_AFTER_M.get(j, ()):
                 exp(e)
             chains = [[(blend_d, e), (blend_e, e), (blend_o, e)] for e in EX_AFTER_W.get(j, ())]
-            chains.append([(w_product, j), (w_quantise, j)])
+            chains.append([(w_product, j), (w_regroup, j), (w_quantise, j)] if j in NATURAL else [(w_product, j), (w_quantise, j)])
             chains.extend([[(g_regroup, g), (g_done, g)] for g in GATE_SLOTS.get(j, ())])
             chains.extend([[(blend_d, e), (blend_e, e), (blend_o, e)] for e in EX_AFTER_M.get(j, ())])
             in_turn(chains)

@@ -91,10 +91,10 @@ def tile_nalu_kernel(tc, input_tensor, W_hat, M_hat, gate, out):
             rows = loaded[(tag, n0 // BLOCK * PASSES + c)]
             return rows[:, :, n0 % BLOCK : n0 % BLOCK + width].rearrange("p t (c i) -> p c t i", i=4)
 
-        def by_columns(tag, piece):
+        def by_halves(tag, piece):
             c, n0, width = piece
             rows = loaded[(tag, n0 // BLOCK * PASSES + c)]
-            return rows[:, :, n0 % BLOCK : n0 % BLOCK + width].rearrange("p t n -> p n t")
+            return rows[:, :, n0 % BLOCK : n0 % BLOCK + width].rearrange("p (h u) n -> p u n h", u=2)
 
         def grouped(tile_, lo, width):
             return tile_[:, lo : lo + width, :].rearrange("p (c i) t -> p c t i", i=4)
@@ -121,10 +121,10 @@ def tile_nalu_kernel(tc, input_tensor, W_hat, M_hat, gate, out):
                     )
                     lo += width
                 return flat
-            res = fac.tile([P, words(W_CHUNKS[j]), PACK], F32, tag="t" + tag, name="t" + tag)
+            res = fac.tile([P, 2, words(W_CHUNKS[j]), 2], F32, tag="t" + tag, name="t" + tag)
             lo = 0
             for piece in W_CHUNKS[j]:
-                nc.scalar.activation(out=res[:, lo : lo + piece[2], :], in_=by_columns(tag, piece), func=ACT.Tanh, scale=scale)
+                nc.scalar.activation(out=res[:, :, lo : lo + piece[2], :], in_=by_halves(tag, piece), func=ACT.Tanh, scale=scale)
                 lo += piece[2]
             return res
 
@@ -139,14 +139,16 @@ def tile_nalu_kernel(tc, input_tensor, W_hat, M_hat, gate, out):
             if j in NATURAL:
                 wn[j] = flats[0].tile([P, PACK, n], BF16, tag="wn", name="wn")
                 res = wn[j][:].rearrange("p t n -> p (t n)")
+                halves = "p a b -> p (a b)"
             else:
                 wg[j] = grp.tile([P, n * PACK], BF16, tag="wg", name="wg", align_bytes=64)
-                res = wg[j][:]
+                res = wg[j][:].rearrange("p (m u) -> p m u", u=2)
+                halves = "p u n h -> p (n h) u"
             nc.vector.scalar_tensor_tensor(
                 out=res,
-                in0=t2[j][:].rearrange("p a b -> p (a b)"),
+                in0=t2[j][:].rearrange(halves),
                 scalar=1.0,
-                in1=t1[j][:].rearrange("p a b -> p (a b)"),
+                in1=t1[j][:].rearrange(halves),
                 op0=ALU.add,
                 op1=ALU.mult,
             )

@@ -43,8 +43,7 @@ UNITS = (
     + ((1280, 128, (0, 1, 2, 3), 10, 10), (1408, 128, (0, 1, 2, 3), 12, 11))
 )
 RAW_BUFS = 5
-NATURAL = (2,)
-GATE_SLOTS = {2: (4, 5), 3: (6,), 4: (7, 8), 5: (9,), 7: (10,), 8: (11,)}
+GATE_SLOTS = {2: (7,), 3: (8,), 4: (9, 10), 5: (11,)}
 TH_AFTER_W = {3: (0,), 4: (2,), 7: (4,), 8: (6,), 9: (8,), 12: (10,)}
 TH_AFTER_M = {3: (1,), 4: (3,), 7: (5,), 8: (7,), 9: (9,), 12: (11,)}
 EX_AFTER_W = {5: (0,), 6: (1, 2), 7: (3,), 9: (4,), 11: (8,)}
@@ -60,7 +59,7 @@ def tile_nalu_kernel(tc, input_tensor, W_hat, M_hat, gate, out):
         fac = ctx.enter_context(tc.tile_pool(name="fac", bufs=3))
         grp = ctx.enter_context(tc.tile_pool(name="grp", bufs=2))
         wq = ctx.enter_context(tc.tile_pool(name="wq", bufs=8))
-        gq = ctx.enter_context(tc.tile_pool(name="gq", bufs=7))
+        gq = ctx.enter_context(tc.tile_pool(name="gq", bufs=len(G_CHUNKS)))
         psz = ctx.enter_context(tc.psum_pool(name="psz", bufs=2))
         psa = ctx.enter_context(tc.psum_pool(name="psa", bufs=3))
         ctx.enter_context(tc.manual_schedule())
@@ -106,21 +105,9 @@ def tile_nalu_kernel(tc, input_tensor, W_hat, M_hat, gate, out):
         t2 = {}
         gg = {}
         wg = {}
-        wn = {}
-        flats = []
         where = {}
 
         def tanh_pass(j, tag, scale):
-            if j in NATURAL:
-                flat = fac.tile([P, PACK, words(W_CHUNKS[j])], F32, tag="t" + tag, name="t" + tag)
-                lo = 0
-                for c, n0, width in W_CHUNKS[j]:
-                    rows = loaded[(tag, n0 // BLOCK * PASSES + c)]
-                    nc.scalar.activation(
-                        out=flat[:, :, lo : lo + width], in_=rows[:, :, n0 % BLOCK : n0 % BLOCK + width], func=ACT.Tanh, scale=scale
-                    )
-                    lo += width
-                return flat
             res = fac.tile([P, 2, words(W_CHUNKS[j]), 2], F32, tag="t" + tag, name="t" + tag)
             lo = 0
             for piece in W_CHUNKS[j]:
@@ -135,29 +122,15 @@ def tile_nalu_kernel(tc, input_tensor, W_hat, M_hat, gate, out):
             t2[j] = tanh_pass(j, "mh", 0.5)
 
         def w_product(j):
-            n = words(W_CHUNKS[j])
-            if j in NATURAL:
-                wn[j] = flats[0].tile([P, PACK, n], BF16, tag="wn", name="wn")
-                res = wn[j][:].rearrange("p t n -> p (t n)")
-                halves = "p a b -> p (a b)"
-            else:
-                wg[j] = grp.tile([P, n * PACK], BF16, tag="wg", name="wg", align_bytes=64)
-                res = wg[j][:].rearrange("p (m u) -> p m u", u=2)
-                halves = "p u n h -> p (n h) u"
+            wg[j] = grp.tile([P, words(W_CHUNKS[j]) * PACK], BF16, tag="wg", name="wg", align_bytes=64)
             nc.vector.scalar_tensor_tensor(
-                out=res,
-                in0=t2[j][:].rearrange(halves),
+                out=wg[j][:].rearrange("p (m u) -> p m u", u=2),
+                in0=t2[j][:].rearrange("p u n h -> p (n h) u"),
                 scalar=1.0,
-                in1=t1[j][:].rearrange(halves),
+                in1=t1[j][:].rearrange("p u n h -> p (n h) u"),
                 op0=ALU.add,
                 op1=ALU.mult,
             )
-
-        def w_regroup(j):
-            n = words(W_CHUNKS[j])
-            wide = grp.tile([P, n, PACK], BF16, tag="wg", name="wg", align_bytes=64)
-            nc.vector.tensor_copy(out=grouped(wide, 0, n), in_=wn[j][:].rearrange("p t (c i) -> p c t i", i=4))
-            wg[j] = wide[:].rearrange("p n t -> p (n t)")
 
         def quantise(kind, pool, chunk, values):
             n = words(chunk)
@@ -242,9 +215,8 @@ def tile_nalu_kernel(tc, input_tensor, W_hat, M_hat, gate, out):
                         c = 2 * half + c2
                         for u in range(2):
                             nc.tensor.transpose(xt[:, c2, u, :], pairs[:, 256 * c + u : 256 * (c + 1) : 2], ident[:])
-                    nc.vector.tensor_copy(
-                        out=xg_pairs[:, 2 * half : 2 * half + 2], in_=xt[:].rearrange("p c u r -> p c r u")
-                    )
+                    copy = nc.scalar.copy if i < 2 else nc.vector.tensor_copy
+                    copy(out=xg_pairs[:, 2 * half : 2 * half + 2], in_=xt[:].rearrange("p c u r -> p c r u"))
 
             def x_quantise(i):
                 nc.vector.quantize_mx(out=x_codes[:, i, :].bitcast(FP8X4), scales=x_scales[:, i, :], in_=xg[i][:])
@@ -262,65 +234,81 @@ def tile_nalu_kernel(tc, input_tensor, W_hat, M_hat, gate, out):
                 nc.vector.quantize_mx(out=l_codes[:, i, :].bitcast(FP8X4), scales=l_scales[:, i, :], in_=lg[i][:])
 
             load(W_hat, "wh", 0)
-            x_load(0)
+            load(gate, "gr", 0)
             load(M_hat, "mh", 0)
-            x_load(1)
+            load(gate, "gr", 1)
             load(W_hat, "wh", 1)
-            x_load(2)
+            x_load(0)
             load(M_hat, "mh", 1)
+            x_load(1)
+            x_load(2)
+            tanh_w(0)
+            g_regroup(0)
+            g_quantise(0)
+            tanh_m(0)
+            g_regroup(1)
+            tanh_w(1)
+            w_product(0)
+            g_quantise(1)
             x_transpose(0)
             x_load(3)
-            load(gate, "gr", 0)
-            load(gate, "gr", 1)
-            load(W_hat, "wh", 2)
-            load(M_hat, "mh", 2)
             load(gate, "gr", 2)
             load(gate, "gr", 3)
-            for k in range(3, RAW_BUFS):
-                load(W_hat, "wh", k)
-                load(M_hat, "mh", k)
             load(gate, "gr", 4)
-
-            tanh_w(0)
-            tanh_m(0)
-            tanh_w(1)
+            load(W_hat, "wh", 2)
+            load(M_hat, "mh", 2)
+            load(gate, "gr", 5)
+            load(gate, "gr", 6)
+            load(W_hat, "wh", 3)
+            load(M_hat, "mh", 3)
+            w_quantise(0)
             tanh_m(1)
-            load(W_hat, "wh", RAW_BUFS)
-            load(M_hat, "mh", RAW_BUFS)
-            load(W_hat, "wh", RAW_BUFS + 1)
-            load(M_hat, "mh", RAW_BUFS + 1)
-            x_transpose(1)
             x_quantise(0)
+            x_transpose(1)
             x_abs(0)
-            w_product(0)
             x_transpose(2)
+            w_product(1)
             x_quantise(1)
             x_abs(1)
-            w_quantise(0)
+            w_quantise(1)
             x_transpose(3)
             x_quantise(2)
             x_abs(2)
-            w_product(1)
             x_quantise(3)
             x_abs(3)
-            w_quantise(1)
             for i in range(ROW_TILES):
                 x_log(i)
-            for g in range(4):
-                g_regroup(g)
-                if g > 0:
-                    g_quantise(g - 1)
-                l_quantise(g)
+            g_regroup(2)
+            load(gate, "gr", 7)
+            load(W_hat, "wh", 4)
+            load(M_hat, "mh", 4)
+            l_quantise(0)
+            g_quantise(2)
+            g_regroup(3)
+            load(gate, "gr", 8)
+            load(W_hat, "wh", 5)
+            load(M_hat, "mh", 5)
+            l_quantise(1)
             g_quantise(3)
-            for g in range(4):
-                load(gate, "gr", RAW_BUFS + g)
+            g_regroup(4)
+            load(gate, "gr", 9)
+            load(W_hat, "wh", 6)
+            load(M_hat, "mh", 6)
+            l_quantise(2)
+            g_quantise(4)
+            g_regroup(5)
+            load(gate, "gr", 10)
+            l_quantise(3)
+            g_quantise(5)
+            g_regroup(6)
+            load(gate, "gr", 11)
+            g_quantise(6)
         state["w"] = 1
-        state["g"] = 3
+        state["g"] = 6
 
         epi = ctx.enter_context(tc.tile_pool(name="epi", bufs=3))
         outs = ctx.enter_context(tc.tile_pool(name="outs", bufs=5))
         gates = ctx.enter_context(tc.tile_pool(name="gates", bufs=6))
-        flats.append(ctx.enter_context(tc.tile_pool(name="flat", bufs=2)))
         th = {}
         m = {}
         d = {}
@@ -385,7 +373,7 @@ def tile_nalu_kernel(tc, input_tensor, W_hat, M_hat, gate, out):
             for e in EX_AFTER_M.get(j, ()):
                 exp(e)
             chains = [[(blend_d, e), (blend_e, e), (blend_o, e)] for e in EX_AFTER_W.get(j, ())]
-            chains.append([(w_product, j), (w_regroup, j), (w_quantise, j)] if j in NATURAL else [(w_product, j), (w_quantise, j)])
+            chains.append([(w_product, j), (w_quantise, j)])
             chains.extend([[(g_regroup, g), (g_done, g)] for g in GATE_SLOTS.get(j, ())])
             chains.extend([[(blend_d, e), (blend_e, e), (blend_o, e)] for e in EX_AFTER_M.get(j, ())])
             in_turn(chains)

@@ -22,32 +22,27 @@ BLOCK = 512
 EPS = 1e-07
 FLOPS = 3 * 2 * B * IN * OUT
 
-WIDE = tuple(((c, b * BLOCK, BLOCK),) for b in range(2) for c in range(PASSES))
-W_CHUNKS = WIDE + (
-    ((0, 1024, 256), (1, 1024, 256)),
-    ((2, 1024, 256), (3, 1024, 256)),
-    ((0, 1280, 128), (1, 1280, 128), (2, 1280, 128), (3, 1280, 128)),
-    ((0, 1408, 128), (1, 1408, 128)),
-    ((2, 1408, 128), (3, 1408, 128)),
+W_CHUNKS = (
+    tuple(((c, 0, BLOCK),) for c in range(PASSES))
+    + tuple(((c, n0, 256), (c + 1, n0, 256)) for n0 in (512, 768, 1024) for c in (0, 2))
+    + (tuple((c, 1280, 128) for c in range(PASSES)),)
+    + (((0, 1408, 128), (1, 1408, 128)), ((2, 1408, 128), (3, 1408, 128)))
 )
-G_CHUNKS = WIDE + (
-    ((0, 1024, 256), (1, 1024, 256)),
-    ((2, 1024, 256), (3, 1024, 256)),
-    ((0, 1280, 128), (1, 1280, 128), (2, 1280, 128), (3, 1280, 128)),
-    ((0, 1408, 128), (1, 1408, 128), (2, 1408, 128), (3, 1408, 128)),
-)
+G_CHUNKS = tuple(((c, b * BLOCK, BLOCK),) for b in range(OUT // BLOCK) for c in range(PASSES))
 UNITS = (
-    tuple((0, 512, (i,), 3, 3) for i in range(ROW_TILES))
-    + tuple((512, 512, (i,), 7, 7) for i in range(ROW_TILES))
-    + ((1024, 256, (0, 1), 9, 9), (1024, 256, (2, 3), 9, 9))
-    + ((1280, 128, (0, 1, 2, 3), 10, 10), (1408, 128, (0, 1, 2, 3), 12, 11))
+    tuple((0, BLOCK, (i,)) for i in range(ROW_TILES))
+    + tuple((n0, 256, rows) for n0 in (512, 768, 1024) for rows in ((0, 1), (2, 3)))
+    + ((1280, 128, (0, 1, 2, 3)), (1408, 128, (0, 1)), (1408, 128, (2, 3)))
 )
 RAW_BUFS = 5
-GATE_SLOTS = {2: (7,), 3: (8,), 4: (9, 10), 5: (11,)}
-TH_AFTER_W = {3: (0,), 4: (2,), 7: (4,), 8: (6,), 9: (8,), 12: (10,)}
-TH_AFTER_M = {3: (1,), 4: (3,), 7: (5,), 8: (7,), 9: (9,), 12: (11,)}
-EX_AFTER_W = {5: (0,), 6: (1, 2), 7: (3,), 9: (4,), 11: (8,)}
-EX_AFTER_M = {9: (5, 6), 10: (7,), 12: (9, 10)}
+HEAD_GATES = 7
+X_ON_SCALAR = (0, 1, 2)
+TH_LEAD = 2
+EX_LAG = 4
+
+
+def last_chunk(chunks, n0):
+    return max(j for j, chunk in enumerate(chunks) for c, first, width in chunk if first <= n0 < first + width)
 
 
 def tile_nalu_kernel(tc, input_tensor, W_hat, M_hat, gate, out):
@@ -68,6 +63,8 @@ def tile_nalu_kernel(tc, input_tensor, W_hat, M_hat, gate, out):
         make_identity(nc, ident[:])
         eps = const.tile([P, 1], F32)
         nc.vector.memset(eps[:], EPS)
+        log_half = const.tile([P, 1], F32)
+        nc.vector.memset(log_half[:], 0.5)
 
         x_codes = keep.tile([P, ROW_TILES, PASSES * P], U32, align_bytes=64)
         x_scales = keep.tile([P, ROW_TILES, PASSES * P], U8, align_bytes=64)
@@ -75,25 +72,32 @@ def tile_nalu_kernel(tc, input_tensor, W_hat, M_hat, gate, out):
         l_scales = keep.tile([P, ROW_TILES, PASSES * P], U8, align_bytes=64)
 
         loaded = {}
+        sources = {"wh": W_hat, "mh": M_hat, "gr": gate}
+        next_load = {"wh": 0, "mh": 0, "gr": 0}
 
-        def load(src, tag, k):
-            b, c = divmod(k, PASSES)
+        def load_columns(tag, c, n0, width):
             rows = raw.tile([P, PACK, BLOCK], BF16, tag=tag, name=tag)
             nc.sync.dma_start(
-                out=rows[:],
-                in_=src[c * K_PASS : (c + 1) * K_PASS, b * BLOCK : (b + 1) * BLOCK].rearrange("(p t) n -> p t n", t=PACK),
+                out=rows[:, :, :width],
+                in_=sources[tag][c * K_PASS : (c + 1) * K_PASS, n0 : n0 + width].rearrange("(p t) n -> p t n", t=PACK),
             )
-            loaded[(tag, k)] = rows
+            loaded.setdefault((tag, c, n0 // BLOCK), []).append((n0, width, rows))
 
-        def by_runs(tag, piece):
-            c, n0, width = piece
-            rows = loaded[(tag, n0 // BLOCK * PASSES + c)]
-            return rows[:, :, n0 % BLOCK : n0 % BLOCK + width].rearrange("p t (c i) -> p c t i", i=4)
+        def load(tag, pieces=1):
+            b, c = divmod(next_load[tag], PASSES)
+            next_load[tag] += 1
+            for q in range(pieces):
+                load_columns(tag, c, b * BLOCK + q * (BLOCK // pieces), BLOCK // pieces)
 
-        def by_halves(tag, piece):
+        def parts(tag, piece):
             c, n0, width = piece
-            rows = loaded[(tag, n0 // BLOCK * PASSES + c)]
-            return rows[:, :, n0 % BLOCK : n0 % BLOCK + width].rearrange("p (h u) n -> p u n h", u=2)
+            res = []
+            for first, w, rows in loaded[(tag, c, n0 // BLOCK)]:
+                lo = max(n0, first)
+                hi = min(n0 + width, first + w)
+                if lo < hi:
+                    res.append((lo - n0, hi - lo, rows[:, :, lo - first : hi - first]))
+            return res
 
         def grouped(tile_, lo, width):
             return tile_[:, lo : lo + width, :].rearrange("p (c i) t -> p c t i", i=4)
@@ -111,7 +115,13 @@ def tile_nalu_kernel(tc, input_tensor, W_hat, M_hat, gate, out):
             res = fac.tile([P, 2, words(W_CHUNKS[j]), 2], F32, tag="t" + tag, name="t" + tag)
             lo = 0
             for piece in W_CHUNKS[j]:
-                nc.scalar.activation(out=res[:, :, lo : lo + piece[2], :], in_=by_halves(tag, piece), func=ACT.Tanh, scale=scale)
+                for off, width, rows in parts(tag, piece):
+                    nc.scalar.activation(
+                        out=res[:, :, lo + off : lo + off + width, :],
+                        in_=rows.rearrange("p (h u) n -> p u n h", u=2),
+                        func=ACT.Tanh,
+                        scale=scale,
+                    )
                 lo += piece[2]
             return res
 
@@ -145,19 +155,24 @@ def tile_nalu_kernel(tc, input_tensor, W_hat, M_hat, gate, out):
 
         def w_quantise(j):
             quantise("w", wq, W_CHUNKS[j], wg[j][:])
+            state["w"] = j
 
         def g_regroup(j):
             gg[j] = grp.tile([P, BLOCK, PACK], BF16, tag="gg", name="gg", align_bytes=64)
             lo = 0
             for piece in G_CHUNKS[j]:
-                nc.vector.tensor_copy(out=grouped(gg[j], lo, piece[2]), in_=by_runs("gr", piece))
+                for off, width, rows in parts("gr", piece):
+                    nc.vector.tensor_copy(
+                        out=grouped(gg[j], lo + off, width), in_=rows.rearrange("p t (c i) -> p c t i", i=4)
+                    )
                 lo += piece[2]
 
         def g_quantise(j):
             quantise("g", gq, G_CHUNKS[j], gg[j][:].rearrange("p n t -> p (n t)"))
+            state["g"] = j
 
         def product(acc, lhs_codes, lhs_scales, kind, e):
-            n0, width, rows = UNITS[e][:3]
+            n0, width, rows = UNITS[e]
             for q, i in enumerate(rows):
                 for c in range(PASSES):
                     cod, sca, lo = where[(kind, c, n0)]
@@ -171,26 +186,31 @@ def tile_nalu_kernel(tc, input_tensor, W_hat, M_hat, gate, out):
                         stop=(c == PASSES - 1),
                     )
 
+        def unit_words(e):
+            return UNITS[e][1] * len(UNITS[e][2])
+
+        W_LAST = [last_chunk(W_CHUNKS, n0) for n0, width, rows in UNITS]
+        G_LAST = [last_chunk(G_CHUNKS, n0) for n0, width, rows in UNITS]
         z = {}
         s2 = {}
         a2 = {}
-        state = {"z": 0, "sa": 0, "th": -1, "ex": -1, "d": -1, "w": -1, "g": -1}
+        state = {"z": 0, "sa": 0, "th": -1, "ex": -1, "q": -1, "w": -1, "g": -1}
 
-        def pe_ready():
+        def pe_ready(w):
             go = True
             while go:
                 go = False
                 e = state["sa"]
-                if e < min(len(UNITS), state["z"]) and UNITS[e][3] <= state["w"] and e - 3 <= min(state["ex"], state["d"]):
-                    s2[e] = psa.tile([P, BLOCK], F32, tag="s", name="s")
+                if e < min(len(UNITS), state["z"]) and W_LAST[e] <= w and e - 3 <= min(state["ex"], state["q"]):
+                    s2[e] = psa.tile([P, unit_words(e)], F32, tag="s", name="s")
                     product(s2[e], l_codes, l_scales, "w", e)
-                    a2[e] = psa.tile([P, BLOCK], F32, tag="a", name="a")
+                    a2[e] = psa.tile([P, unit_words(e)], F32, tag="a", name="a")
                     product(a2[e], x_codes, x_scales, "w", e)
                     state["sa"] = e + 1
                     go = True
                 e = state["z"]
-                if e < len(UNITS) and UNITS[e][4] <= state["g"] and e - 2 <= state["th"]:
-                    z[e] = psz.tile([P, BLOCK], F32, tag="z", name="z")
+                if e < len(UNITS) and G_LAST[e] <= state["g"] and e - 2 <= state["th"]:
+                    z[e] = psz.tile([P, unit_words(e)], F32, tag="z", name="z")
                     product(z[e], x_codes, x_scales, "g", e)
                     state["z"] = e + 1
                     go = True
@@ -215,7 +235,7 @@ def tile_nalu_kernel(tc, input_tensor, W_hat, M_hat, gate, out):
                         c = 2 * half + c2
                         for u in range(2):
                             nc.tensor.transpose(xt[:, c2, u, :], pairs[:, 256 * c + u : 256 * (c + 1) : 2], ident[:])
-                    copy = nc.scalar.copy if i < 2 else nc.vector.tensor_copy
+                    copy = nc.scalar.copy if i in X_ON_SCALAR else nc.vector.tensor_copy
                     copy(out=xg_pairs[:, 2 * half : 2 * half + 2], in_=xt[:].rearrange("p c u r -> p c r u"))
 
             def x_quantise(i):
@@ -233,13 +253,13 @@ def tile_nalu_kernel(tc, input_tensor, W_hat, M_hat, gate, out):
             def l_quantise(i):
                 nc.vector.quantize_mx(out=l_codes[:, i, :].bitcast(FP8X4), scales=l_scales[:, i, :], in_=lg[i][:])
 
-            load(W_hat, "wh", 0)
-            load(gate, "gr", 0)
-            load(M_hat, "mh", 0)
-            load(gate, "gr", 1)
-            load(W_hat, "wh", 1)
+            load("wh", 1)
+            load("gr", 1)
+            load("mh")
+            load("gr")
+            load("wh")
             x_load(0)
-            load(M_hat, "mh", 1)
+            load("mh")
             x_load(1)
             x_load(2)
             tanh_w(0)
@@ -252,15 +272,10 @@ def tile_nalu_kernel(tc, input_tensor, W_hat, M_hat, gate, out):
             g_quantise(1)
             x_transpose(0)
             x_load(3)
-            load(gate, "gr", 2)
-            load(gate, "gr", 3)
-            load(gate, "gr", 4)
-            load(W_hat, "wh", 2)
-            load(M_hat, "mh", 2)
-            load(gate, "gr", 5)
-            load(gate, "gr", 6)
-            load(W_hat, "wh", 3)
-            load(M_hat, "mh", 3)
+            load("gr")
+            load("gr")
+            load("wh")
+            load("mh")
             w_quantise(0)
             tanh_m(1)
             x_quantise(0)
@@ -272,116 +287,126 @@ def tile_nalu_kernel(tc, input_tensor, W_hat, M_hat, gate, out):
             x_abs(1)
             w_quantise(1)
             x_transpose(3)
+            load("gr")
+            load("wh")
+            load("mh")
+            load("gr")
             x_quantise(2)
             x_abs(2)
             x_quantise(3)
             x_abs(3)
             for i in range(ROW_TILES):
                 x_log(i)
-            g_regroup(2)
-            load(gate, "gr", 7)
-            load(W_hat, "wh", 4)
-            load(M_hat, "mh", 4)
-            l_quantise(0)
-            g_quantise(2)
-            g_regroup(3)
-            load(gate, "gr", 8)
-            load(W_hat, "wh", 5)
-            load(M_hat, "mh", 5)
-            l_quantise(1)
-            g_quantise(3)
-            g_regroup(4)
-            load(gate, "gr", 9)
-            load(W_hat, "wh", 6)
-            load(M_hat, "mh", 6)
-            l_quantise(2)
-            g_quantise(4)
-            g_regroup(5)
-            load(gate, "gr", 10)
-            l_quantise(3)
-            g_quantise(5)
-            g_regroup(6)
-            load(gate, "gr", 11)
-            g_quantise(6)
-        state["w"] = 1
-        state["g"] = 6
+            nc.scalar.activation(out=log_half[:], in_=log_half[:], func=ACT.Ln)
+            logs = 0
+            for g in range(2, HEAD_GATES):
+                g_regroup(g)
+                if next_load["gr"] < len(G_CHUNKS):
+                    load("gr")
+                if next_load["wh"] < 6:
+                    load("wh")
+                    load("mh")
+                if logs < ROW_TILES:
+                    l_quantise(logs)
+                    logs += 1
+                g_quantise(g)
+            for i in range(logs, ROW_TILES):
+                l_quantise(i)
+
 
         epi = ctx.enter_context(tc.tile_pool(name="epi", bufs=3))
         outs = ctx.enter_context(tc.tile_pool(name="outs", bufs=5))
         gates = ctx.enter_context(tc.tile_pool(name="gates", bufs=6))
         th = {}
         m = {}
-        d = {}
+        ga = {}
 
         def gate_tanh(e):
-            th[e] = gates.tile([P, BLOCK], F32, tag="th", name="th")
+            th[e] = gates.tile([P, unit_words(e)], F32, tag="th", name="th")
             nc.scalar.activation(out=th[e][:], in_=z[e][:], func=ACT.Tanh, scale=0.5)
             state["th"] = e
-            pe_ready()
 
         def exp(e):
-            m[e] = outs.tile([P, BLOCK], F32, tag="m", name="m")
-            nc.scalar.activation(out=m[e][:], in_=s2[e][:], func=ACT.Exp, scale=0.5)
+            m[e] = outs.tile([P, unit_words(e)], F32, tag="m", name="m")
+            nc.scalar.activation(out=m[e][:], in_=s2[e][:], func=ACT.Exp, bias=log_half[:], scale=0.5)
             state["ex"] = e
 
-        def blend_d(e):
-            d[e] = epi.tile([P, BLOCK], F32, tag="d", name="d")
-            nc.vector.scalar_tensor_tensor(
-                out=d[e][:], in0=a2[e][:], scalar=0.5, in1=m[e][:], op0=ALU.mult, op1=ALU.subtract
-            )
-            state["d"] = e
-            pe_ready()
+        def blend_q(e):
+            ga[e] = epi.tile([P, unit_words(e)], F32, tag="ga", name="ga")
+            nc.vector.scalar_tensor_tensor(out=ga[e][:], in0=th[e][:], scalar=1.0, in1=a2[e][:], op0=ALU.add, op1=ALU.mult)
+            state["q"] = e
 
-        def blend_e(e):
-            nc.vector.scalar_tensor_tensor(out=d[e][:], in0=th[e][:], scalar=1.0, in1=d[e][:], op0=ALU.add, op1=ALU.mult)
+        def blend_r(e):
+            nc.vector.scalar_tensor_tensor(out=m[e][:], in0=th[e][:], scalar=1.0, in1=m[e][:], op0=ALU.subtract, op1=ALU.mult)
 
         def blend_o(e):
-            n0, width, rows = UNITS[e][:3]
-            nc.vector.scalar_tensor_tensor(out=m[e][:], in0=d[e][:], scalar=0.5, in1=m[e][:], op0=ALU.mult, op1=ALU.add)
+            n0, width, rows = UNITS[e]
+            nc.vector.scalar_tensor_tensor(out=m[e][:], in0=ga[e][:], scalar=0.25, in1=m[e][:], op0=ALU.mult, op1=ALU.subtract)
             nc.sync.dma_start(
                 out=out[rows[0] * P : (rows[-1] + 1) * P, n0 : n0 + width].rearrange("(i p) n -> p i n", p=P),
                 in_=m[e][:].rearrange("p (i n) -> p i n", n=width),
             )
-
-        def g_done(g):
-            g_quantise(g)
-            state["g"] = g
-            pe_ready()
 
         def in_turn(chains):
             for step in range(max(len(chain) for chain in chains)):
                 for chain in chains:
                     if step < len(chain):
                         chain[step][0](chain[step][1])
+                        pe_ready(PE_HOLD[0])
 
+        PE_HOLD = [1]
+        pe_ready(1)
+        EX_AT = {}
+        TH_AT = {}
+        place = th_place = 0
+        for e in range(len(UNITS)):
+            place = max(place + 1, 2 * (W_LAST[e] + 1) + EX_LAG)
+            EX_AT.setdefault(place, []).append(e)
+            th_place = max(th_place + 1, place - TH_LEAD, 2 * 2 + 1)
+            TH_AT.setdefault(th_place, []).append(e)
+        last_use = {}
+        for j, chunk in enumerate(W_CHUNKS):
+            for c, n0, width in chunk:
+                last_use[n0 // BLOCK * PASSES + c] = j
         n_loads = OUT // BLOCK * PASSES
-        pe_ready()
+        gates_done = HEAD_GATES
         for j in range(2, len(W_CHUNKS)):
             tanh_w(j)
-            for e in TH_AFTER_W.get(j, ()):
+            for e in TH_AT.get(2 * j, ()):
                 gate_tanh(e)
-            for e in EX_AFTER_W.get(j, ()):
+                pe_ready(j - 2)
+            for e in EX_AT.get(2 * j, ()):
                 exp(e)
             tanh_m(j)
-            if j + RAW_BUFS < n_loads:
-                load(W_hat, "wh", j + RAW_BUFS)
-                load(M_hat, "mh", j + RAW_BUFS)
-            for e in TH_AFTER_M.get(j, ()):
+            while next_load["wh"] < n_loads and last_use[next_load["wh"] - RAW_BUFS + 0] <= j:
+                load("wh")
+                load("mh")
+            for e in TH_AT.get(2 * j + 1, ()):
                 gate_tanh(e)
-            state["w"] = j - 1
-            pe_ready()
-            for e in EX_AFTER_M.get(j, ()):
+                pe_ready(j - 2)
+            PE_HOLD[0] = j - 1
+            pe_ready(j - 1)
+            for e in EX_AT.get(2 * j + 1, ()):
                 exp(e)
-            chains = [[(blend_d, e), (blend_e, e), (blend_o, e)] for e in EX_AFTER_W.get(j, ())]
-            chains.append([(w_product, j), (w_quantise, j)])
-            chains.extend([[(g_regroup, g), (g_done, g)] for g in GATE_SLOTS.get(j, ())])
-            chains.extend([[(blend_d, e), (blend_e, e), (blend_o, e)] for e in EX_AFTER_M.get(j, ())])
+            chains = [[(blend_q, e), (blend_r, e), (blend_o, e)] for e in EX_AT.get(2 * j, ())]
+            chains.insert(0 if j >= 11 else len(chains), [(w_product, j), (w_quantise, j)])
+            gs = range(gates_done, min(len(G_CHUNKS), gates_done + {0: 1}.get(j, 1)))
+            gates_done += len(gs)
+            chains.extend([[(g_regroup, g), (g_quantise, g)] for g in gs])
+            chains.extend([[(blend_q, e), (blend_r, e), (blend_o, e)] for e in EX_AT.get(2 * j + 1, ())])
             in_turn(chains)
-            for g in GATE_SLOTS.get(j, ()):
-                if g + RAW_BUFS < n_loads:
-                    load(gate, "gr", g + RAW_BUFS)
-        state["w"] = len(W_CHUNKS) - 1
-        pe_ready()
-        for e in range(state["ex"] + 1, len(UNITS)):
+            for g in gs:
+                if next_load["gr"] < n_loads:
+                    load("gr")
+        first = state["ex"] + 1
+        for e in range(state["th"] + 1, len(UNITS)):
+            pe_ready(len(W_CHUNKS) - 2)
+            gate_tanh(e)
+        for e in range(first, len(UNITS)):
+            pe_ready(state["w"])
             exp(e)
-            in_turn([[(blend_d, e), (blend_e, e), (blend_o, e)]])
+            blend_r(e)
+            if e > first:
+                blend_o(e - 1)
+            blend_q(e)
+        blend_o(len(UNITS) - 1)

@@ -35,10 +35,10 @@ UNITS = (
     + ((1280, 128, (0, 1, 2, 3)), (1408, 128, (0, 1)), (1408, 128, (2, 3)))
 )
 RAW_BUFS = 5
-HEAD_GATES = 7
-X_ON_SCALAR = (0, 1, 2)
-TH_LEAD = 2
-EX_LAG = 4
+HEAD_GATES = 8
+X_ON_SCALAR = (0, 1, 2, 3)
+TH_LEAD = 4
+EX_LAG = 1280
 
 
 def last_chunk(chunks, n0):
@@ -54,7 +54,7 @@ def tile_nalu_kernel(tc, input_tensor, W_hat, M_hat, gate, out):
         fac = ctx.enter_context(tc.tile_pool(name="fac", bufs=3))
         grp = ctx.enter_context(tc.tile_pool(name="grp", bufs=2))
         wq = ctx.enter_context(tc.tile_pool(name="wq", bufs=8))
-        gq = ctx.enter_context(tc.tile_pool(name="gq", bufs=len(G_CHUNKS)))
+        gq = ctx.enter_context(tc.tile_pool(name="gq", bufs=12))
         psz = ctx.enter_context(tc.psum_pool(name="psz", bufs=2))
         psa = ctx.enter_context(tc.psum_pool(name="psa", bufs=3))
         ctx.enter_context(tc.manual_schedule())
@@ -65,6 +65,7 @@ def tile_nalu_kernel(tc, input_tensor, W_hat, M_hat, gate, out):
         nc.vector.memset(eps[:], EPS)
         log_half = const.tile([P, 1], F32)
         nc.vector.memset(log_half[:], 0.5)
+        nc.scalar.activation(out=log_half[:], in_=log_half[:], func=ACT.Ln)
 
         x_codes = keep.tile([P, ROW_TILES, PASSES * P], U32, align_bytes=64)
         x_scales = keep.tile([P, ROW_TILES, PASSES * P], U8, align_bytes=64)
@@ -112,7 +113,7 @@ def tile_nalu_kernel(tc, input_tensor, W_hat, M_hat, gate, out):
         where = {}
 
         def tanh_pass(j, tag, scale):
-            res = fac.tile([P, 2, words(W_CHUNKS[j]), 2], F32, tag="t" + tag, name="t" + tag)
+            res = fac.tile([P, 2, words(W_CHUNKS[j]), 2], F32, tag="t" + tag, name="t" + tag, bufs=3 if tag == "wh" else 2)
             lo = 0
             for piece in W_CHUNKS[j]:
                 for off, width, rows in parts(tag, piece):
@@ -215,19 +216,23 @@ def tile_nalu_kernel(tc, input_tensor, W_hat, M_hat, gate, out):
                     state["z"] = e + 1
                     go = True
 
-        with tc.tile_pool(name="xin", bufs=3) as xin, tc.tile_pool(name="xwork", bufs=4) as xwork:
+        with tc.tile_pool(name="xin", bufs=ROW_TILES) as xin, tc.tile_pool(name="xwork", bufs=4) as xwork:
             x_sb = {}
+            x_banks = {}
             xg = {}
             lg = {}
 
-            def x_load(i):
+            def x_load(i, pieces=1):
                 x_sb[i] = xin.tile([P, IN], BF16, tag="x_sb", name="x_sb")
-                nc.sync.dma_start(out=x_sb[i][:], in_=input_tensor[i * P : (i + 1) * P, :])
+                n = IN // pieces
+                for q in range(pieces):
+                    nc.sync.dma_start(
+                        out=x_sb[i][:, q * n : (q + 1) * n], in_=input_tensor[i * P : (i + 1) * P, q * n : (q + 1) * n]
+                    )
 
             def x_transpose(i):
                 pairs = x_sb[i][:].bitcast(F32)
                 xg[i] = xwork.tile([P, PASSES * P * PACK], BF16, tag="xg", name="xg", align_bytes=64)
-                xg_pairs = xg[i][:].bitcast(F32).rearrange("p (c r u) -> p c r u", c=PASSES, u=2)
                 for half in range(PASSES // 2):
                     pool, tag = ((psa, "s"), (psa, "a"), (psz, "z"))[(2 * i + half) % 3]
                     xt = pool.tile([P, 2, 2, P], F32, tag=tag, name=tag)
@@ -235,81 +240,93 @@ def tile_nalu_kernel(tc, input_tensor, W_hat, M_hat, gate, out):
                         c = 2 * half + c2
                         for u in range(2):
                             nc.tensor.transpose(xt[:, c2, u, :], pairs[:, 256 * c + u : 256 * (c + 1) : 2], ident[:])
-                    copy = nc.scalar.copy if i in X_ON_SCALAR else nc.vector.tensor_copy
+                    x_banks[(i, half)] = xt
+
+            def x_copy(i):
+                xg_pairs = xg[i][:].bitcast(F32).rearrange("p (c r u) -> p c r u", c=PASSES, u=2)
+                copy = nc.scalar.copy if i in X_ON_SCALAR else nc.vector.tensor_copy
+                for half in range(PASSES // 2):
+                    xt = x_banks[(i, half)]
                     copy(out=xg_pairs[:, 2 * half : 2 * half + 2], in_=xt[:].rearrange("p c u r -> p c r u"))
 
             def x_quantise(i):
                 nc.vector.quantize_mx(out=x_codes[:, i, :].bitcast(FP8X4), scales=x_scales[:, i, :], in_=xg[i][:])
 
-            def x_abs(i):
+            def x_abs(i, q=0, pieces=1):
+                n = PASSES * P * PACK // pieces
+                if q == 0:
+                    lg[i] = xwork.tile([P, PASSES * P * PACK], BF16, tag="lg", name="lg", align_bytes=64)
+                part = slice(q * n // 2, (q + 1) * n // 2)
                 nc.vector.tensor_single_scalar(
-                    out=xg[i][:].bitcast(I32), in_=xg[i][:].bitcast(I32), scalar=0x7FFF7FFF, op=ALU.bitwise_and
+                    out=lg[i][:].bitcast(I32)[:, part], in_=xg[i][:].bitcast(I32)[:, part], scalar=0x7FFF7FFF, op=ALU.bitwise_and
                 )
 
-            def x_log(i):
-                lg[i] = xwork.tile([P, PASSES * P * PACK], BF16, tag="lg", name="lg", align_bytes=64)
-                nc.scalar.activation(out=lg[i][:], in_=xg[i][:], func=ACT.Ln, bias=eps[:], scale=1.0)
+            def x_log(i, q=0, pieces=1):
+                n = PASSES * P * PACK // pieces
+                part = lg[i][:, q * n : (q + 1) * n]
+                nc.scalar.activation(out=part, in_=part, func=ACT.Ln, bias=eps[:], scale=1.0)
 
             def l_quantise(i):
                 nc.vector.quantize_mx(out=l_codes[:, i, :].bitcast(FP8X4), scales=l_scales[:, i, :], in_=lg[i][:])
 
-            load("wh", 1)
-            load("gr", 1)
-            load("mh")
+            x_load(0, 2)
             load("gr")
-            load("wh")
-            x_load(0)
-            load("mh")
             x_load(1)
             x_load(2)
-            tanh_w(0)
-            g_regroup(0)
-            g_quantise(0)
-            tanh_m(0)
-            g_regroup(1)
-            tanh_w(1)
-            w_product(0)
-            g_quantise(1)
-            x_transpose(0)
+            load("gr")
             x_load(3)
             load("gr")
             load("gr")
-            load("wh")
-            load("mh")
-            w_quantise(0)
-            tanh_m(1)
-            x_quantise(0)
-            x_transpose(1)
-            x_abs(0)
-            x_transpose(2)
-            w_product(1)
-            x_quantise(1)
-            x_abs(1)
-            w_quantise(1)
-            x_transpose(3)
             load("gr")
             load("wh")
             load("mh")
-            load("gr")
-            x_quantise(2)
-            x_abs(2)
-            x_quantise(3)
-            x_abs(3)
             for i in range(ROW_TILES):
-                x_log(i)
-            nc.scalar.activation(out=log_half[:], in_=log_half[:], func=ACT.Ln)
-            logs = 0
-            for g in range(2, HEAD_GATES):
+                x_transpose(i)
+            x_copy(0)
+            x_abs(0, 0, 2)
+            x_log(0, 0, 2)
+            x_abs(0, 1, 2)
+            x_log(0, 1, 2)
+            g_regroup(0)
+            load("gr")
+            x_copy(1)
+            x_quantise(0)
+            g_quantise(0)
+            x_copy(2)
+            g_regroup(1)
+            load("gr")
+            x_abs(1)
+            x_log(1)
+            x_quantise(1)
+            x_abs(2)
+            x_copy(3)
+            x_log(2)
+            g_quantise(1)
+            g_regroup(2)
+            load("gr")
+            load("wh")
+            load("mh")
+            x_quantise(2)
+            x_abs(3)
+            x_log(3)
+            g_quantise(2)
+            x_quantise(3)
+            l_quantise(0)
+            logs = 1
+            for g in range(3, HEAD_GATES):
                 g_regroup(g)
                 if next_load["gr"] < len(G_CHUNKS):
                     load("gr")
-                if next_load["wh"] < 6:
+                if next_load["wh"] < RAW_BUFS and g % 2 == 1:
                     load("wh")
                     load("mh")
                 if logs < ROW_TILES:
                     l_quantise(logs)
                     logs += 1
                 g_quantise(g)
+            while next_load["wh"] < RAW_BUFS:
+                load("wh")
+                load("mh")
             for i in range(logs, ROW_TILES):
                 l_quantise(i)
 
@@ -354,15 +371,21 @@ def tile_nalu_kernel(tc, input_tensor, W_hat, M_hat, gate, out):
                         chain[step][0](chain[step][1])
                         pe_ready(PE_HOLD[0])
 
-        PE_HOLD = [1]
-        pe_ready(1)
+        PE_HOLD = [-1]
+        pe_ready(-1)
         EX_AT = {}
         TH_AT = {}
         place = th_place = 0
+        issued = []
+        for chunk in W_CHUNKS:
+            for half in range(2):
+                issued.append((issued[-1] if issued else 0) + words(chunk))
         for e in range(len(UNITS)):
-            place = max(place + 1, 2 * (W_LAST[e] + 1) + EX_LAG)
+            place = max(place + 1, 2 * (W_LAST[e] + 1) + 1)
+            while place < len(issued) and issued[place] - issued[2 * W_LAST[e] + 1] < EX_LAG:
+                place += 1
             EX_AT.setdefault(place, []).append(e)
-            th_place = max(th_place + 1, place - TH_LEAD, 2 * 2 + 1)
+            th_place = max(th_place + 1, place - TH_LEAD)
             TH_AT.setdefault(th_place, []).append(e)
         last_use = {}
         for j, chunk in enumerate(W_CHUNKS):
@@ -370,7 +393,8 @@ def tile_nalu_kernel(tc, input_tensor, W_hat, M_hat, gate, out):
                 last_use[n0 // BLOCK * PASSES + c] = j
         n_loads = OUT // BLOCK * PASSES
         gates_done = HEAD_GATES
-        for j in range(2, len(W_CHUNKS)):
+        late = []
+        for j in range(len(W_CHUNKS)):
             tanh_w(j)
             for e in TH_AT.get(2 * j, ()):
                 gate_tanh(e)
@@ -378,7 +402,7 @@ def tile_nalu_kernel(tc, input_tensor, W_hat, M_hat, gate, out):
             for e in EX_AT.get(2 * j, ()):
                 exp(e)
             tanh_m(j)
-            while next_load["wh"] < n_loads and last_use[next_load["wh"] - RAW_BUFS + 0] <= j:
+            while next_load["wh"] < n_loads and (next_load["wh"] < RAW_BUFS or last_use[next_load["wh"] - RAW_BUFS] <= j):
                 load("wh")
                 load("mh")
             for e in TH_AT.get(2 * j + 1, ()):
@@ -388,17 +412,21 @@ def tile_nalu_kernel(tc, input_tensor, W_hat, M_hat, gate, out):
             pe_ready(j - 1)
             for e in EX_AT.get(2 * j + 1, ()):
                 exp(e)
-            chains = [[(blend_q, e), (blend_r, e), (blend_o, e)] for e in EX_AT.get(2 * j, ())]
+            chains = [[(blend_q, e), (blend_r, e), (blend_o, e)] for e in late + EX_AT.get(2 * j, [])]
+            late = EX_AT.get(2 * j + 1, [])
+            if not False:
+                chains.extend([[(blend_q, e), (blend_r, e), (blend_o, e)] for e in late])
+                late = []
             chains.insert(0 if j >= 11 else len(chains), [(w_product, j), (w_quantise, j)])
-            gs = range(gates_done, min(len(G_CHUNKS), gates_done + {0: 1}.get(j, 1)))
+            gs = range(gates_done, min(len(G_CHUNKS), gates_done + {1: 0}.get(j, 1)))
             gates_done += len(gs)
             chains.extend([[(g_regroup, g), (g_quantise, g)] for g in gs])
-            chains.extend([[(blend_q, e), (blend_r, e), (blend_o, e)] for e in EX_AT.get(2 * j + 1, ())])
             in_turn(chains)
-            for g in gs:
-                if next_load["gr"] < n_loads:
-                    load("gr")
+            while next_load["gr"] < min(n_loads, gates_done + RAW_BUFS):
+                load("gr")
         first = state["ex"] + 1
+        if late:
+            in_turn([[(blend_q, e), (blend_r, e), (blend_o, e)] for e in late])
         for e in range(state["th"] + 1, len(UNITS)):
             pe_ready(len(W_CHUNKS) - 2)
             gate_tanh(e)

@@ -35,10 +35,9 @@ UNITS = (
     + ((1280, 128, (0, 1, 2, 3)), (1408, 128, (0, 1)), (1408, 128, (2, 3)))
 )
 RAW_BUFS = 5
-HEAD_GATES = 8
-X_ON_SCALAR = (0, 1, 2, 3)
+HEAD_GATES = 6
 TH_LEAD = 4
-EX_LAG = 1280
+EX_LAG = 1536
 
 
 def last_chunk(chunks, n0):
@@ -242,12 +241,12 @@ def tile_nalu_kernel(tc, input_tensor, W_hat, M_hat, gate, out):
                             nc.tensor.transpose(xt[:, c2, u, :], pairs[:, 256 * c + u : 256 * (c + 1) : 2], ident[:])
                     x_banks[(i, half)] = xt
 
-            def x_copy(i):
+            def x_copy(copy, i, q=0, pieces=2):
+                n = PASSES // pieces
                 xg_pairs = xg[i][:].bitcast(F32).rearrange("p (c r u) -> p c r u", c=PASSES, u=2)
-                copy = nc.scalar.copy if i in X_ON_SCALAR else nc.vector.tensor_copy
-                for half in range(PASSES // 2):
-                    xt = x_banks[(i, half)]
-                    copy(out=xg_pairs[:, 2 * half : 2 * half + 2], in_=xt[:].rearrange("p c u r -> p c r u"))
+                lo = q * n
+                xt = x_banks[(i, lo // 2)]
+                copy(out=xg_pairs[:, lo : lo + n], in_=xt[:, lo % 2 : lo % 2 + n].rearrange("p c u r -> p c r u"))
 
             def x_quantise(i):
                 nc.vector.quantize_mx(out=x_codes[:, i, :].bitcast(FP8X4), scales=x_scales[:, i, :], in_=xg[i][:])
@@ -269,9 +268,9 @@ def tile_nalu_kernel(tc, input_tensor, W_hat, M_hat, gate, out):
             def l_quantise(i):
                 nc.vector.quantize_mx(out=l_codes[:, i, :].bitcast(FP8X4), scales=l_scales[:, i, :], in_=lg[i][:])
 
-            x_load(0, 2)
+            x_load(0, 4)
+            x_load(1, 2)
             load("gr")
-            x_load(1)
             x_load(2)
             load("gr")
             x_load(3)
@@ -280,37 +279,51 @@ def tile_nalu_kernel(tc, input_tensor, W_hat, M_hat, gate, out):
             load("gr")
             load("wh")
             load("mh")
+            vec = nc.vector.tensor_copy
+            sca = nc.scalar.copy
             for i in range(ROW_TILES):
                 x_transpose(i)
-            x_copy(0)
-            x_abs(0, 0, 2)
-            x_log(0, 0, 2)
-            x_abs(0, 1, 2)
-            x_log(0, 1, 2)
+            x_copy(vec, 0, 0, 4)
+            x_copy(vec, 0, 1, 4)
+            x_abs(0, 0, 4)
+            x_log(0, 0, 4)
+            x_copy(vec, 0, 2, 4)
+            x_abs(0, 1, 4)
+            x_log(0, 1, 4)
+            x_copy(vec, 0, 3, 4)
+            x_abs(0, 2, 4)
+            x_log(0, 2, 4)
+            x_abs(0, 3, 4)
+            x_log(0, 3, 4)
+            x_copy(sca, 1, 1)
+            x_copy(vec, 1, 0)
+            x_abs(1, 0, 2)
+            x_log(1, 0, 2)
+            x_abs(1, 1, 2)
+            x_log(1, 1, 2)
+            x_quantise(0)
             g_regroup(0)
             load("gr")
-            x_copy(1)
-            x_quantise(0)
+            x_copy(sca, 2, 0)
+            x_copy(sca, 2, 1)
+            x_quantise(1)
             g_quantise(0)
-            x_copy(2)
+            x_abs(2)
+            x_copy(sca, 3, 0)
+            x_copy(sca, 3, 1)
+            x_log(2)
             g_regroup(1)
             load("gr")
-            x_abs(1)
-            x_log(1)
-            x_quantise(1)
-            x_abs(2)
-            x_copy(3)
-            x_log(2)
+            x_quantise(2)
+            x_abs(3)
+            x_log(3)
             g_quantise(1)
             g_regroup(2)
             load("gr")
             load("wh")
             load("mh")
-            x_quantise(2)
-            x_abs(3)
-            x_log(3)
-            g_quantise(2)
             x_quantise(3)
+            g_quantise(2)
             l_quantise(0)
             logs = 1
             for g in range(3, HEAD_GATES):
@@ -393,6 +406,7 @@ def tile_nalu_kernel(tc, input_tensor, W_hat, M_hat, gate, out):
                 last_use[n0 // BLOCK * PASSES + c] = j
         n_loads = OUT // BLOCK * PASSES
         gates_done = HEAD_GATES
+        GPS = {0: 2}
         late = []
         for j in range(len(W_CHUNKS)):
             tanh_w(j)
@@ -417,8 +431,8 @@ def tile_nalu_kernel(tc, input_tensor, W_hat, M_hat, gate, out):
             if not False:
                 chains.extend([[(blend_q, e), (blend_r, e), (blend_o, e)] for e in late])
                 late = []
-            chains.insert(0 if j >= 11 else len(chains), [(w_product, j), (w_quantise, j)])
-            gs = range(gates_done, min(len(G_CHUNKS), gates_done + {1: 0}.get(j, 1)))
+            chains.insert(0 if j >= 0 else len(chains), [(w_product, j), (w_quantise, j)])
+            gs = range(gates_done, min(len(G_CHUNKS), gates_done + GPS.get(j, 1)))
             gates_done += len(gs)
             chains.extend([[(g_regroup, g), (g_quantise, g)] for g in gs])
             in_turn(chains)

@@ -28,13 +28,16 @@ W_CHUNKS = (
     + (tuple((c, 1280, 128) for c in range(PASSES)),)
     + (((0, 1408, 128), (1, 1408, 128)), ((2, 1408, 128), (3, 1408, 128)))
 )
-G_CHUNKS = tuple(((c, b * BLOCK, BLOCK),) for b in range(OUT // BLOCK) for c in range(PASSES))
+G_CHUNKS = tuple(
+    tuple((c, b * BLOCK, BLOCK) for c in range(c0, c0 + 1)) for b in range(OUT // BLOCK) for c0 in range(0, PASSES, 1)
+)
 UNITS = (
     tuple((0, BLOCK, (i,)) for i in range(ROW_TILES))
     + tuple((n0, 256, rows) for n0 in (512, 768, 1024) for rows in ((0, 1), (2, 3)))
     + ((1280, 128, (0, 1, 2, 3)), (1408, 128, (0, 1)), (1408, 128, (2, 3)))
 )
 RAW_BUFS = 5
+RUN = 8
 HEAD_GATES = 6
 TH_LEAD = 4
 EX_LAG = 1536
@@ -100,7 +103,7 @@ def tile_nalu_kernel(tc, input_tensor, W_hat, M_hat, gate, out):
             return res
 
         def grouped(tile_, lo, width):
-            return tile_[:, lo : lo + width, :].rearrange("p (c i) t -> p c t i", i=4)
+            return tile_[:, lo : lo + width, :].rearrange("p (c i) t -> p c t i", i=RUN)
 
         def words(chunk):
             return sum(width for c, n0, width in chunk)
@@ -158,12 +161,12 @@ def tile_nalu_kernel(tc, input_tensor, W_hat, M_hat, gate, out):
             state["w"] = j
 
         def g_regroup(j):
-            gg[j] = grp.tile([P, BLOCK, PACK], BF16, tag="gg", name="gg", align_bytes=64)
+            gg[j] = grp.tile([P, words(G_CHUNKS[j]), PACK], BF16, tag="gg", name="gg", align_bytes=64)
             lo = 0
             for piece in G_CHUNKS[j]:
                 for off, width, rows in parts("gr", piece):
                     nc.vector.tensor_copy(
-                        out=grouped(gg[j], lo + off, width), in_=rows.rearrange("p t (c i) -> p c t i", i=4)
+                        out=grouped(gg[j], lo + off, width), in_=rows.rearrange("p t (c i) -> p c t i", i=RUN)
                     )
                 lo += piece[2]
 
@@ -229,24 +232,22 @@ def tile_nalu_kernel(tc, input_tensor, W_hat, M_hat, gate, out):
                         out=x_sb[i][:, q * n : (q + 1) * n], in_=input_tensor[i * P : (i + 1) * P, q * n : (q + 1) * n]
                     )
 
-            def x_transpose(i):
+            def x_transpose(i, pieces=2):
                 pairs = x_sb[i][:].bitcast(F32)
                 xg[i] = xwork.tile([P, PASSES * P * PACK], BF16, tag="xg", name="xg", align_bytes=64)
-                for half in range(PASSES // 2):
-                    pool, tag = ((psa, "s"), (psa, "a"), (psz, "z"))[(2 * i + half) % 3]
-                    xt = pool.tile([P, 2, 2, P], F32, tag=tag, name=tag)
-                    for c2 in range(2):
-                        c = 2 * half + c2
+                n = PASSES // pieces
+                for q in range(pieces):
+                    pool, tag = ((psa, "s"), (psa, "a"), (psz, "z"))[len(x_banks) % 3 if len(x_banks) < 8 else len(x_banks) % 8]
+                    xt = pool.tile([P, n, 2, P], F32, tag=tag, name=tag)
+                    x_banks[(i, q)] = xt
+                    for c in range(q * n, (q + 1) * n):
                         for u in range(2):
-                            nc.tensor.transpose(xt[:, c2, u, :], pairs[:, 256 * c + u : 256 * (c + 1) : 2], ident[:])
-                    x_banks[(i, half)] = xt
+                            nc.tensor.transpose(xt[:, c - q * n, u, :], pairs[:, 256 * c + u : 256 * (c + 1) : 2], ident[:])
 
             def x_copy(copy, i, q=0, pieces=2):
                 n = PASSES // pieces
                 xg_pairs = xg[i][:].bitcast(F32).rearrange("p (c r u) -> p c r u", c=PASSES, u=2)
-                lo = q * n
-                xt = x_banks[(i, lo // 2)]
-                copy(out=xg_pairs[:, lo : lo + n], in_=xt[:, lo % 2 : lo % 2 + n].rearrange("p c u r -> p c r u"))
+                copy(out=xg_pairs[:, q * n : (q + 1) * n], in_=x_banks[(i, q)][:].rearrange("p c u r -> p c r u"))
 
             def x_quantise(i):
                 nc.vector.quantize_mx(out=x_codes[:, i, :].bitcast(FP8X4), scales=x_scales[:, i, :], in_=xg[i][:])
@@ -282,7 +283,7 @@ def tile_nalu_kernel(tc, input_tensor, W_hat, M_hat, gate, out):
             vec = nc.vector.tensor_copy
             sca = nc.scalar.copy
             for i in range(ROW_TILES):
-                x_transpose(i)
+                x_transpose(i, 4 if i == 0 else 2)
             x_copy(vec, 0, 0, 4)
             x_copy(vec, 0, 1, 4)
             x_abs(0, 0, 4)
@@ -295,10 +296,10 @@ def tile_nalu_kernel(tc, input_tensor, W_hat, M_hat, gate, out):
             x_log(0, 2, 4)
             x_abs(0, 3, 4)
             x_log(0, 3, 4)
-            x_copy(sca, 1, 1)
             x_copy(vec, 1, 0)
             x_abs(1, 0, 2)
             x_log(1, 0, 2)
+            x_copy(vec, 1, 1)
             x_abs(1, 1, 2)
             x_log(1, 1, 2)
             x_quantise(0)
@@ -407,7 +408,6 @@ def tile_nalu_kernel(tc, input_tensor, W_hat, M_hat, gate, out):
         n_loads = OUT // BLOCK * PASSES
         gates_done = HEAD_GATES
         GPS = {0: 2}
-        late = []
         for j in range(len(W_CHUNKS)):
             tanh_w(j)
             for e in TH_AT.get(2 * j, ()):
@@ -426,12 +426,9 @@ def tile_nalu_kernel(tc, input_tensor, W_hat, M_hat, gate, out):
             pe_ready(j - 1)
             for e in EX_AT.get(2 * j + 1, ()):
                 exp(e)
-            chains = [[(blend_q, e), (blend_r, e), (blend_o, e)] for e in late + EX_AT.get(2 * j, [])]
-            late = EX_AT.get(2 * j + 1, [])
-            if not False:
-                chains.extend([[(blend_q, e), (blend_r, e), (blend_o, e)] for e in late])
-                late = []
-            chains.insert(0 if j >= 0 else len(chains), [(w_product, j), (w_quantise, j)])
+            chains = [[(blend_q, e), (blend_r, e), (blend_o, e)] for e in EX_AT.get(2 * j, ())]
+            chains.extend([[(blend_q, e), (blend_r, e), (blend_o, e)] for e in EX_AT.get(2 * j + 1, ())])
+            chains.insert(0, [(w_product, j), (w_quantise, j)])
             gs = range(gates_done, min(len(G_CHUNKS), gates_done + GPS.get(j, 1)))
             gates_done += len(gs)
             chains.extend([[(g_regroup, g), (g_quantise, g)] for g in gs])
@@ -439,8 +436,6 @@ def tile_nalu_kernel(tc, input_tensor, W_hat, M_hat, gate, out):
             while next_load["gr"] < min(n_loads, gates_done + RAW_BUFS):
                 load("gr")
         first = state["ex"] + 1
-        if late:
-            in_turn([[(blend_q, e), (blend_r, e), (blend_o, e)] for e in late])
         for e in range(state["th"] + 1, len(UNITS)):
             pe_ready(len(W_CHUNKS) - 2)
             gate_tanh(e)

@@ -204,9 +204,14 @@ def tile_nalu_kernel(tc, input_tensor, W_hat, M_hat, gate, out):
             while go:
                 go = False
                 e = state["sa"]
-                if e < min(len(UNITS), state["z"]) and W_LAST[e] <= w and e - 3 <= min(state["ex"], state["q"]):
+                ready = []
+                while len(ready) < 2 and e < min(len(UNITS), state["z"]) and W_LAST[e] <= w and e - 3 <= min(state["ex"], state["q"]):
+                    ready.append(e)
+                    e += 1
+                for e in ready:
                     s2[e] = psa.tile([P, unit_words(e)], F32, tag="s", name="s")
                     product(s2[e], l_codes, l_scales, "w", e)
+                for e in ready:
                     a2[e] = psa.tile([P, unit_words(e)], F32, tag="a", name="a")
                     product(a2[e], x_codes, x_scales, "w", e)
                     state["sa"] = e + 1
@@ -218,11 +223,13 @@ def tile_nalu_kernel(tc, input_tensor, W_hat, M_hat, gate, out):
                     state["z"] = e + 1
                     go = True
 
-        with tc.tile_pool(name="xin", bufs=ROW_TILES) as xin, tc.tile_pool(name="xwork", bufs=4) as xwork:
+        with tc.tile_pool(name="xin", bufs=ROW_TILES) as xin, tc.tile_pool(name="xwork", bufs=2) as xwork:
             x_sb = {}
             x_banks = {}
             xg = {}
             lg = {}
+            xgs = []
+            lgs = []
 
             def x_load(i, pieces=1):
                 x_sb[i] = xin.tile([P, IN], BF16, tag="x_sb", name="x_sb")
@@ -234,7 +241,14 @@ def tile_nalu_kernel(tc, input_tensor, W_hat, M_hat, gate, out):
 
             def x_transpose(i, pieces=2):
                 pairs = x_sb[i][:].bitcast(F32)
-                xg[i] = xwork.tile([P, PASSES * P * PACK], BF16, tag="xg", name="xg", align_bytes=64)
+                if i % 2 == 0:
+                    xg_pair = xwork.tile([P, 2, PASSES * P * PACK], BF16, tag="xg", name="xg", align_bytes=64)
+                    lg_pair = xwork.tile([P, 2, PASSES * P * PACK], BF16, tag="lg", name="lg", align_bytes=64)
+                    for q in range(2):
+                        xg[i + q] = xg_pair[:, q, :]
+                        lg[i + q] = lg_pair[:, q, :]
+                    xgs.append(xg_pair)
+                    lgs.append(lg_pair)
                 n = PASSES // pieces
                 for q in range(pieces):
                     pool, tag = ((psa, "s"), (psa, "a"), (psz, "z"))[len(x_banks) % 3 if len(x_banks) < 8 else len(x_banks) % 8]
@@ -246,19 +260,23 @@ def tile_nalu_kernel(tc, input_tensor, W_hat, M_hat, gate, out):
 
             def x_copy(copy, i, q=0, pieces=2):
                 n = PASSES // pieces
-                xg_pairs = xg[i][:].bitcast(F32).rearrange("p (c r u) -> p c r u", c=PASSES, u=2)
+                xg_pairs = xg[i].bitcast(F32).rearrange("p (c r u) -> p c r u", c=PASSES, u=2)
                 copy(out=xg_pairs[:, q * n : (q + 1) * n], in_=x_banks[(i, q)][:].rearrange("p c u r -> p c r u"))
 
-            def x_quantise(i):
-                nc.vector.quantize_mx(out=x_codes[:, i, :].bitcast(FP8X4), scales=x_scales[:, i, :], in_=xg[i][:])
+            def flat(ap):
+                return ap.rearrange("p i n -> p (i n)")
+
+            def x_quantise(h):
+                two = slice(2 * h, 2 * h + 2)
+                nc.vector.quantize_mx(
+                    out=flat(x_codes[:, two, :]).bitcast(FP8X4), scales=flat(x_scales[:, two, :]), in_=flat(xgs[h][:])
+                )
 
             def x_abs(i, q=0, pieces=1):
                 n = PASSES * P * PACK // pieces
-                if q == 0:
-                    lg[i] = xwork.tile([P, PASSES * P * PACK], BF16, tag="lg", name="lg", align_bytes=64)
                 part = slice(q * n // 2, (q + 1) * n // 2)
                 nc.vector.tensor_single_scalar(
-                    out=lg[i][:].bitcast(I32)[:, part], in_=xg[i][:].bitcast(I32)[:, part], scalar=0x7FFF7FFF, op=ALU.bitwise_and
+                    out=lg[i].bitcast(I32)[:, part], in_=xg[i].bitcast(I32)[:, part], scalar=0x7FFF7FFF, op=ALU.bitwise_and
                 )
 
             def x_log(i, q=0, pieces=1):
@@ -266,8 +284,11 @@ def tile_nalu_kernel(tc, input_tensor, W_hat, M_hat, gate, out):
                 part = lg[i][:, q * n : (q + 1) * n]
                 nc.scalar.activation(out=part, in_=part, func=ACT.Ln, bias=eps[:], scale=1.0)
 
-            def l_quantise(i):
-                nc.vector.quantize_mx(out=l_codes[:, i, :].bitcast(FP8X4), scales=l_scales[:, i, :], in_=lg[i][:])
+            def l_quantise(h):
+                two = slice(2 * h, 2 * h + 2)
+                nc.vector.quantize_mx(
+                    out=flat(l_codes[:, two, :]).bitcast(FP8X4), scales=flat(l_scales[:, two, :]), in_=flat(lgs[h][:])
+                )
 
             x_load(0, 4)
             x_load(1, 2)
@@ -296,18 +317,17 @@ def tile_nalu_kernel(tc, input_tensor, W_hat, M_hat, gate, out):
             x_log(0, 2, 4)
             x_abs(0, 3, 4)
             x_log(0, 3, 4)
+            x_copy(sca, 1, 1)
             x_copy(vec, 1, 0)
             x_abs(1, 0, 2)
             x_log(1, 0, 2)
-            x_copy(vec, 1, 1)
             x_abs(1, 1, 2)
             x_log(1, 1, 2)
-            x_quantise(0)
             g_regroup(0)
             load("gr")
             x_copy(sca, 2, 0)
             x_copy(sca, 2, 1)
-            x_quantise(1)
+            x_quantise(0)
             g_quantise(0)
             x_abs(2)
             x_copy(sca, 3, 0)
@@ -315,7 +335,6 @@ def tile_nalu_kernel(tc, input_tensor, W_hat, M_hat, gate, out):
             x_log(2)
             g_regroup(1)
             load("gr")
-            x_quantise(2)
             x_abs(3)
             x_log(3)
             g_quantise(1)
@@ -323,10 +342,10 @@ def tile_nalu_kernel(tc, input_tensor, W_hat, M_hat, gate, out):
             load("gr")
             load("wh")
             load("mh")
-            x_quantise(3)
+            x_quantise(1)
             g_quantise(2)
             l_quantise(0)
-            logs = 1
+            logs = 2
             for g in range(3, HEAD_GATES):
                 g_regroup(g)
                 if next_load["gr"] < len(G_CHUNKS):
@@ -334,15 +353,15 @@ def tile_nalu_kernel(tc, input_tensor, W_hat, M_hat, gate, out):
                 if next_load["wh"] < RAW_BUFS and g % 2 == 1:
                     load("wh")
                     load("mh")
-                if logs < ROW_TILES:
-                    l_quantise(logs)
-                    logs += 1
+                if logs == 2 and g == 4:
+                    l_quantise(1)
+                    logs = ROW_TILES
                 g_quantise(g)
             while next_load["wh"] < RAW_BUFS:
                 load("wh")
                 load("mh")
-            for i in range(logs, ROW_TILES):
-                l_quantise(i)
+            if logs < ROW_TILES:
+                l_quantise(1)
 
 
         epi = ctx.enter_context(tc.tile_pool(name="epi", bufs=3))

@@ -205,7 +205,7 @@ def tile_nalu_kernel(tc, input_tensor, W_hat, M_hat, gate, out):
                 go = False
                 e = state["sa"]
                 ready = []
-                while len(ready) < 2 and e < min(len(UNITS), state["z"]) and W_LAST[e] <= w and e - 3 <= min(state["ex"], state["q"]):
+                while len(ready) < (2 if e + 1 < len(UNITS) - 1 else 1) and e < min(len(UNITS), state["z"]) and W_LAST[e] <= w and e - 3 <= min(state["ex"], state["q"]):
                     ready.append(e)
                     e += 1
                 for e in ready:

@@ -22,25 +22,31 @@ BLOCK = 512
 EPS = 1e-07
 FLOPS = 3 * 2 * B * IN * OUT
 
-W_CHUNKS = (
-    tuple(((c, 0, BLOCK),) for c in range(PASSES))
-    + tuple(((c, n0, 256), (c + 1, n0, 256)) for n0 in (512, 768, 1024) for c in (0, 2))
-    + (tuple((c, 1280, 128) for c in range(PASSES)),)
-    + (((0, 1408, 128), (1, 1408, 128)), ((2, 1408, 128), (3, 1408, 128)))
+HALVES = (0, 256, 512, 768, 1024)
+NARROW = (1280, 1408)
+W_CHUNKS = tuple(
+    ((c, n0, width), (c + 1, n0, width))
+    for blocks, width in ((HALVES, 256), (NARROW, 128))
+    for n0 in blocks
+    for c in range(0, PASSES, 2)
 )
 G_CHUNKS = tuple(
     tuple((c, b * BLOCK, BLOCK) for c in range(c0, c0 + 1)) for b in range(OUT // BLOCK) for c0 in range(0, PASSES, 1)
 )
 UNITS = (
-    tuple((0, BLOCK, (i,)) for i in range(ROW_TILES))
-    + tuple((n0, 256, rows) for n0 in (512, 768, 1024) for rows in ((0, 1), (2, 3)))
+    tuple((n0, 256, rows) for n0 in HALVES for rows in ((0, 1), (2, 3)))
     + ((1280, 128, (0, 1, 2, 3)), (1408, 128, (0, 1)), (1408, 128, (2, 3)))
 )
-RAW_BUFS = 5
+RAW_BUFS = 7
+GATE_BUFS = 5
 RUN = 8
+WQ_BUFS = 8
+HEAD_LOADS = ("gr", "2", "gr", "3", "gr", "wh", "wh", "gr", "mh", "mh", "gr", "wh", "mh", "wh", "mh")
 HEAD_GATES = 6
-TH_LEAD = 4
-EX_LAG = 1536
+TH_LEAD = 2
+EX_LAG = 1408
+EX_STEP = 2
+SLOT_GATES = (1, 1, 1, 0, 1, 1, 1)
 
 
 def last_chunk(chunks, n0):
@@ -52,10 +58,9 @@ def tile_nalu_kernel(tc, input_tensor, W_hat, M_hat, gate, out):
     with ExitStack() as ctx:
         const = ctx.enter_context(tc.tile_pool(name="const", bufs=1))
         keep = ctx.enter_context(tc.tile_pool(name="keep", bufs=1))
-        raw = ctx.enter_context(tc.tile_pool(name="raw", bufs=RAW_BUFS))
+        raw = ctx.enter_context(tc.tile_pool(name="raw", bufs=1))
         fac = ctx.enter_context(tc.tile_pool(name="fac", bufs=3))
         grp = ctx.enter_context(tc.tile_pool(name="grp", bufs=2))
-        wq = ctx.enter_context(tc.tile_pool(name="wq", bufs=8))
         gq = ctx.enter_context(tc.tile_pool(name="gq", bufs=12))
         psz = ctx.enter_context(tc.psum_pool(name="psz", bufs=2))
         psa = ctx.enter_context(tc.psum_pool(name="psa", bufs=3))
@@ -79,7 +84,7 @@ def tile_nalu_kernel(tc, input_tensor, W_hat, M_hat, gate, out):
         next_load = {"wh": 0, "mh": 0, "gr": 0}
 
         def load_columns(tag, c, n0, width):
-            rows = raw.tile([P, PACK, BLOCK], BF16, tag=tag, name=tag)
+            rows = raw.tile([P, PACK, BLOCK], BF16, tag=tag, name=tag, bufs=GATE_BUFS if tag == "gr" else RAW_BUFS)
             nc.sync.dma_start(
                 out=rows[:, :, :width],
                 in_=sources[tag][c * K_PASS : (c + 1) * K_PASS, n0 : n0 + width].rearrange("(p t) n -> p t n", t=PACK),
@@ -292,15 +297,11 @@ def tile_nalu_kernel(tc, input_tensor, W_hat, M_hat, gate, out):
 
             x_load(0, 4)
             x_load(1, 2)
-            load("gr")
-            x_load(2)
-            load("gr")
-            x_load(3)
-            load("gr")
-            load("gr")
-            load("gr")
-            load("wh")
-            load("mh")
+            for item in HEAD_LOADS:
+                if item in ("gr", "wh", "mh"):
+                    load(item)
+                else:
+                    x_load(int(item))
             vec = nc.vector.tensor_copy
             sca = nc.scalar.copy
             for i in range(ROW_TILES):
@@ -324,7 +325,6 @@ def tile_nalu_kernel(tc, input_tensor, W_hat, M_hat, gate, out):
             x_abs(1, 1, 2)
             x_log(1, 1, 2)
             g_regroup(0)
-            load("gr")
             x_copy(sca, 2, 0)
             x_copy(sca, 2, 1)
             x_quantise(0)
@@ -334,36 +334,26 @@ def tile_nalu_kernel(tc, input_tensor, W_hat, M_hat, gate, out):
             x_copy(sca, 3, 1)
             x_log(2)
             g_regroup(1)
-            load("gr")
             x_abs(3)
             x_log(3)
             g_quantise(1)
             g_regroup(2)
-            load("gr")
-            load("wh")
-            load("mh")
             x_quantise(1)
             g_quantise(2)
             l_quantise(0)
             logs = 2
             for g in range(3, HEAD_GATES):
                 g_regroup(g)
-                if next_load["gr"] < len(G_CHUNKS):
-                    load("gr")
-                if next_load["wh"] < RAW_BUFS and g % 2 == 1:
-                    load("wh")
-                    load("mh")
+                load("gr")
                 if logs == 2 and g == 4:
                     l_quantise(1)
                     logs = ROW_TILES
                 g_quantise(g)
-            while next_load["wh"] < RAW_BUFS:
-                load("wh")
-                load("mh")
             if logs < ROW_TILES:
                 l_quantise(1)
 
 
+        wq = ctx.enter_context(tc.tile_pool(name="wq", bufs=WQ_BUFS))
         epi = ctx.enter_context(tc.tile_pool(name="epi", bufs=3))
         outs = ctx.enter_context(tc.tile_pool(name="outs", bufs=5))
         gates = ctx.enter_context(tc.tile_pool(name="gates", bufs=6))
@@ -397,14 +387,6 @@ def tile_nalu_kernel(tc, input_tensor, W_hat, M_hat, gate, out):
                 in_=m[e][:].rearrange("p (i n) -> p i n", n=width),
             )
 
-        def in_turn(chains):
-            for step in range(max(len(chain) for chain in chains)):
-                for chain in chains:
-                    if step < len(chain):
-                        chain[step][0](chain[step][1])
-                        pe_ready(PE_HOLD[0])
-
-        PE_HOLD = [-1]
         pe_ready(-1)
         EX_AT = {}
         TH_AT = {}
@@ -414,7 +396,7 @@ def tile_nalu_kernel(tc, input_tensor, W_hat, M_hat, gate, out):
             for half in range(2):
                 issued.append((issued[-1] if issued else 0) + words(chunk))
         for e in range(len(UNITS)):
-            place = max(place + 1, 2 * (W_LAST[e] + 1) + 1)
+            place = max(place + EX_STEP, 2 * (W_LAST[e] + 1) + 1)
             while place < len(issued) and issued[place] - issued[2 * W_LAST[e] + 1] < EX_LAG:
                 place += 1
             EX_AT.setdefault(place, []).append(e)
@@ -426,7 +408,20 @@ def tile_nalu_kernel(tc, input_tensor, W_hat, M_hat, gate, out):
                 last_use[n0 // BLOCK * PASSES + c] = j
         n_loads = OUT // BLOCK * PASSES
         gates_done = HEAD_GATES
-        GPS = {0: 2}
+        late = []
+        def load_ahead(j):
+            go = True
+            while go:
+                go = False
+                if next_load["wh"] < n_loads and (next_load["wh"] < RAW_BUFS or last_use[next_load["wh"] - RAW_BUFS] <= j):
+                    load("wh")
+                    load("mh")
+                    go = True
+                if next_load["gr"] < min(n_loads, gates_done + GATE_BUFS):
+                    load("gr")
+                    go = True
+
+        load_ahead(-1)
         for j in range(len(W_CHUNKS)):
             tanh_w(j)
             for e in TH_AT.get(2 * j, ()):
@@ -435,25 +430,24 @@ def tile_nalu_kernel(tc, input_tensor, W_hat, M_hat, gate, out):
             for e in EX_AT.get(2 * j, ()):
                 exp(e)
             tanh_m(j)
-            while next_load["wh"] < n_loads and (next_load["wh"] < RAW_BUFS or last_use[next_load["wh"] - RAW_BUFS] <= j):
-                load("wh")
-                load("mh")
             for e in TH_AT.get(2 * j + 1, ()):
                 gate_tanh(e)
                 pe_ready(j - 2)
-            PE_HOLD[0] = j - 1
             pe_ready(j - 1)
             for e in EX_AT.get(2 * j + 1, ()):
                 exp(e)
-            chains = [[(blend_q, e), (blend_r, e), (blend_o, e)] for e in EX_AT.get(2 * j, ())]
-            chains.extend([[(blend_q, e), (blend_r, e), (blend_o, e)] for e in EX_AT.get(2 * j + 1, ())])
-            chains.insert(0, [(w_product, j), (w_quantise, j)])
-            gs = range(gates_done, min(len(G_CHUNKS), gates_done + GPS.get(j, 1)))
-            gates_done += len(gs)
-            chains.extend([[(g_regroup, g), (g_quantise, g)] for g in gs])
-            in_turn(chains)
-            while next_load["gr"] < min(n_loads, gates_done + RAW_BUFS):
-                load("gr")
+            units = EX_AT.get(2 * j, []) + EX_AT.get(2 * j + 1, [])
+            fresh = range(gates_done, min(len(G_CHUNKS), gates_done + (SLOT_GATES[j] if j < len(SLOT_GATES) else 0)))
+            gates_done += len(fresh)
+            ops = [(blend_o, e) for e in late] + [(g_regroup, g) for g in fresh] + [(blend_q, e) for e in units]
+            ops += [(w_product, j)] + [(blend_r, e) for e in units] + [(g_quantise, g) for g in fresh] + [(w_quantise, j)]
+            late = units
+            for op, which in ops:
+                op(which)
+                pe_ready(j - 1)
+            load_ahead(j)
+        for e in late:
+            blend_o(e)
         first = state["ex"] + 1
         for e in range(state["th"] + 1, len(UNITS)):
             pe_ready(len(W_CHUNKS) - 2)

@@ -22,9 +22,9 @@ BLOCK = 512
 EPS = 1e-07
 FLOPS = 3 * 2 * B * IN * OUT
 
-HALVES = (0, 256, 512, 768, 1024)
+HALVES = (512, 768, 1024)
 NARROW = (1280, 1408)
-W_CHUNKS = tuple(
+W_CHUNKS = tuple(((c, 0, BLOCK),) for c in range(PASSES)) + tuple(
     ((c, n0, width), (c + 1, n0, width))
     for blocks, width in ((HALVES, 256), (NARROW, 128))
     for n0 in blocks
@@ -34,19 +34,19 @@ G_CHUNKS = tuple(
     tuple((c, b * BLOCK, BLOCK) for c in range(c0, c0 + 1)) for b in range(OUT // BLOCK) for c0 in range(0, PASSES, 1)
 )
 UNITS = (
-    tuple((n0, 256, rows) for n0 in HALVES for rows in ((0, 1), (2, 3)))
+    tuple((0, BLOCK, (i,)) for i in range(ROW_TILES))
+    + tuple((n0, 256, rows) for n0 in HALVES for rows in ((0, 1), (2, 3)))
     + ((1280, 128, (0, 1, 2, 3)), (1408, 128, (0, 1)), (1408, 128, (2, 3)))
 )
 RAW_BUFS = 7
 GATE_BUFS = 5
 RUN = 8
 WQ_BUFS = 8
-HEAD_LOADS = ("gr", "2", "gr", "3", "gr", "wh", "wh", "gr", "mh", "mh", "gr", "wh", "mh", "wh", "mh")
-HEAD_GATES = 6
-TH_LEAD = 2
-EX_LAG = 1408
+HEAD_LOADS = ("1", "gr", "2", "gr", "3", "wh", "mh", "gr", "wh", "mh", "gr", "gr")
+HEAD_GATES = 4
+TH_LEAD = 3
+EX_LAG = 1792
 EX_STEP = 2
-SLOT_GATES = (1, 1, 1, 0, 1, 1, 1)
 
 
 def last_chunk(chunks, n0):
@@ -296,12 +296,11 @@ def tile_nalu_kernel(tc, input_tensor, W_hat, M_hat, gate, out):
                 )
 
             x_load(0, 4)
-            x_load(1, 2)
             for item in HEAD_LOADS:
                 if item in ("gr", "wh", "mh"):
                     load(item)
                 else:
-                    x_load(int(item))
+                    x_load(int(item), 2 if item == "1" else 1)
             vec = nc.vector.tensor_copy
             sca = nc.scalar.copy
             for i in range(ROW_TILES):
@@ -309,48 +308,41 @@ def tile_nalu_kernel(tc, input_tensor, W_hat, M_hat, gate, out):
             x_copy(vec, 0, 0, 4)
             x_copy(vec, 0, 1, 4)
             x_abs(0, 0, 4)
-            x_log(0, 0, 4)
             x_copy(vec, 0, 2, 4)
             x_abs(0, 1, 4)
-            x_log(0, 1, 4)
             x_copy(vec, 0, 3, 4)
             x_abs(0, 2, 4)
-            x_log(0, 2, 4)
             x_abs(0, 3, 4)
-            x_log(0, 3, 4)
-            x_copy(sca, 1, 1)
-            x_copy(vec, 1, 0)
+            x_copy(vec, 1, 0, 2)
             x_abs(1, 0, 2)
-            x_log(1, 0, 2)
+            x_log(0, 0, 4)
+            x_log(0, 1, 4)
+            x_log(0, 2, 4)
+            x_log(0, 3, 4)
+            x_copy(sca, 1, 1, 2)
             x_abs(1, 1, 2)
-            x_log(1, 1, 2)
             g_regroup(0)
-            x_copy(sca, 2, 0)
-            x_copy(sca, 2, 1)
-            x_quantise(0)
+            x_copy(vec, 2, 0, 2)
+            x_copy(vec, 2, 1, 2)
             g_quantise(0)
-            x_abs(2)
-            x_copy(sca, 3, 0)
-            x_copy(sca, 3, 1)
-            x_log(2)
+            x_abs(2, 0, 1)
+            x_copy(vec, 3, 0, 2)
+            x_copy(vec, 3, 1, 2)
             g_regroup(1)
-            x_abs(3)
-            x_log(3)
-            g_quantise(1)
-            g_regroup(2)
+            x_abs(3, 0, 1)
+            x_quantise(0)
             x_quantise(1)
-            g_quantise(2)
+            g_quantise(1)
+            x_log(1, 0, 2)
+            x_log(1, 1, 2)
             l_quantise(0)
-            logs = 2
-            for g in range(3, HEAD_GATES):
-                g_regroup(g)
-                load("gr")
-                if logs == 2 and g == 4:
-                    l_quantise(1)
-                    logs = ROW_TILES
-                g_quantise(g)
-            if logs < ROW_TILES:
-                l_quantise(1)
+            g_regroup(2)
+            x_log(2, 0, 1)
+            x_log(3, 0, 1)
+            l_quantise(1)
+            g_quantise(2)
+            g_regroup(3)
+            g_quantise(3)
 
 
         wq = ctx.enter_context(tc.tile_pool(name="wq", bufs=WQ_BUFS))
@@ -437,7 +429,7 @@ def tile_nalu_kernel(tc, input_tensor, W_hat, M_hat, gate, out):
             for e in EX_AT.get(2 * j + 1, ()):
                 exp(e)
             units = EX_AT.get(2 * j, []) + EX_AT.get(2 * j + 1, [])
-            fresh = range(gates_done, min(len(G_CHUNKS), gates_done + (SLOT_GATES[j] if j < len(SLOT_GATES) else 0)))
+            fresh = range(gates_done, min(len(G_CHUNKS), gates_done + 1))
             gates_done += len(fresh)
             ops = [(blend_o, e) for e in late] + [(g_regroup, g) for g in fresh] + [(blend_q, e) for e in units]
             ops += [(w_product, j)] + [(blend_r, e) for e in units] + [(g_quantise, g) for g in fresh] + [(w_quantise, j)]

@@ -42,7 +42,7 @@ RAW_BUFS = 7
 GATE_BUFS = 5
 RUN = 8
 WQ_BUFS = 8
-HEAD_LOADS = ("1", "gr", "2", "gr", "3", "wh", "mh", "gr", "wh", "mh", "gr", "gr")
+HEAD_LOADS = ("1", "2", "gr", "3", "gr", "wh", "mh", "gr", "wh", "mh", "gr", "gr")
 HEAD_GATES = 4
 TH_LEAD = 3
 EX_LAG = 1792
@@ -314,27 +314,27 @@ def tile_nalu_kernel(tc, input_tensor, W_hat, M_hat, gate, out):
             x_abs(0, 2, 4)
             x_abs(0, 3, 4)
             x_copy(vec, 1, 0, 2)
+            x_copy(vec, 1, 1, 2)
             x_abs(1, 0, 2)
+            x_abs(1, 1, 2)
+            g_regroup(0)
+            x_copy(vec, 2, 0, 2)
+            g_quantise(0)
             x_log(0, 0, 4)
             x_log(0, 1, 4)
             x_log(0, 2, 4)
             x_log(0, 3, 4)
-            x_copy(sca, 1, 1, 2)
-            x_abs(1, 1, 2)
-            g_regroup(0)
-            x_copy(vec, 2, 0, 2)
-            x_copy(vec, 2, 1, 2)
-            g_quantise(0)
+            x_log(1, 0, 2)
+            x_copy(sca, 2, 1, 2)
             x_abs(2, 0, 1)
             x_copy(vec, 3, 0, 2)
-            x_copy(vec, 3, 1, 2)
             g_regroup(1)
+            x_log(1, 1, 2)
+            x_copy(sca, 3, 1, 2)
             x_abs(3, 0, 1)
             x_quantise(0)
             x_quantise(1)
             g_quantise(1)
-            x_log(1, 0, 2)
-            x_log(1, 1, 2)
             l_quantise(0)
             g_regroup(2)
             x_log(2, 0, 1)

@@ -44,7 +44,7 @@ RUN = 8
 WQ_BUFS = 8
 HEAD_LOADS = ("1", "2", "gr", "3", "gr", "wh", "mh", "gr", "wh", "mh", "gr", "gr")
 HEAD_GATES = 4
-TH_LEAD = 3
+TH_LEAD = 1
 EX_LAG = 1792
 EX_STEP = 2
 
@@ -317,22 +317,22 @@ def tile_nalu_kernel(tc, input_tensor, W_hat, M_hat, gate, out):
             x_copy(vec, 1, 1, 2)
             x_abs(1, 0, 2)
             x_abs(1, 1, 2)
+            x_quantise(0)
             g_regroup(0)
-            x_copy(vec, 2, 0, 2)
-            g_quantise(0)
             x_log(0, 0, 4)
             x_log(0, 1, 4)
             x_log(0, 2, 4)
             x_log(0, 3, 4)
             x_log(1, 0, 2)
+            x_copy(sca, 2, 0, 2)
             x_copy(sca, 2, 1, 2)
             x_abs(2, 0, 1)
+            g_quantise(0)
             x_copy(vec, 3, 0, 2)
             g_regroup(1)
             x_log(1, 1, 2)
             x_copy(sca, 3, 1, 2)
             x_abs(3, 0, 1)
-            x_quantise(0)
             x_quantise(1)
             g_quantise(1)
             l_quantise(0)
@@ -340,8 +340,8 @@ def tile_nalu_kernel(tc, input_tensor, W_hat, M_hat, gate, out):
             x_log(2, 0, 1)
             x_log(3, 0, 1)
             l_quantise(1)
-            g_quantise(2)
             g_regroup(3)
+            g_quantise(2)
             g_quantise(3)
 
 
@@ -441,10 +441,10 @@ def tile_nalu_kernel(tc, input_tensor, W_hat, M_hat, gate, out):
         for e in late:
             blend_o(e)
         first = state["ex"] + 1
-        for e in range(state["th"] + 1, len(UNITS)):
-            pe_ready(len(W_CHUNKS) - 2)
-            gate_tanh(e)
         for e in range(first, len(UNITS)):
+            pe_ready(len(W_CHUNKS) - 2)
+            if state["th"] < e:
+                gate_tanh(e)
             pe_ready(state["w"])
             exp(e)
             blend_r(e)

from contextlib import ExitStack

import concourse.mybir as mybir
from concourse.masks import make_identity

FP8X4 = mybir.dt.float8_e4m3fn_x4
BF16 = mybir.dt.bfloat16
F32 = mybir.dt.float32
I32 = mybir.dt.int32
U32 = mybir.dt.uint32
U8 = mybir.dt.uint8
ACT = mybir.ActivationFunctionType
ALU = mybir.AluOpType

P = 128
PACK = 4
K_PASS = P * PACK
B, IN, OUT = 512, 2048, 1536
PASSES = IN // K_PASS
ROW_TILES = B // P
BLOCK = 512
EPS = 1e-07
FLOPS = 3 * 2 * B * IN * OUT

HALVES = (512, 768, 1024)
NARROW = (1280, 1408)
W_CHUNKS = tuple(((c, 0, BLOCK),) for c in range(PASSES)) + tuple(
    ((c, n0, width), (c + 1, n0, width))
    for blocks, width in ((HALVES, 256), (NARROW, 128))
    for n0 in blocks
    for c in range(0, PASSES, 2)
)
G_CHUNKS = tuple(
    tuple((c, b * BLOCK, BLOCK) for c in range(c0, c0 + 1)) for b in range(OUT // BLOCK) for c0 in range(0, PASSES, 1)
)
UNITS = (
    tuple((0, BLOCK, (i,)) for i in range(ROW_TILES))
    + tuple((n0, 256, rows) for n0 in HALVES for rows in ((0, 1), (2, 3)))
    + ((1280, 128, (0, 1, 2, 3)), (1408, 128, (0, 1)), (1408, 128, (2, 3)))
)
RAW_BUFS = 7
GATE_BUFS = 5
RUN = 8
WQ_BUFS = 8
HEAD_LOADS = ("1", "2", "gr", "3", "gr", "wh", "mh", "gr", "wh", "mh", "gr", "gr")
HEAD_GATES = 4
TH_LEAD = 1
EX_LAG = 1792
EX_STEP = 2


def last_chunk(chunks, n0):
    return max(j for j, chunk in enumerate(chunks) for c, first, width in chunk if first <= n0 < first + width)


def tile_nalu_kernel(tc, input_tensor, W_hat, M_hat, gate, out):
    nc = tc.nc
    with ExitStack() as ctx:
        const = ctx.enter_context(tc.tile_pool(name="const", bufs=1))
        keep = ctx.enter_context(tc.tile_pool(name="keep", bufs=1))
        raw = ctx.enter_context(tc.tile_pool(name="raw", bufs=1))
        fac = ctx.enter_context(tc.tile_pool(name="fac", bufs=3))
        grp = ctx.enter_context(tc.tile_pool(name="grp", bufs=2))
        gq = ctx.enter_context(tc.tile_pool(name="gq", bufs=12))
        psz = ctx.enter_context(tc.psum_pool(name="psz", bufs=2))
        psa = ctx.enter_context(tc.psum_pool(name="psa", bufs=3))
        ctx.enter_context(tc.manual_schedule())

        ident = const.tile([P, P], F32)
        make_identity(nc, ident[:])
        eps = const.tile([P, 1], F32)
        nc.vector.memset(eps[:], EPS)
        log_half = const.tile([P, 1], F32)
        nc.vector.memset(log_half[:], 0.5)
        nc.scalar.activation(out=log_half[:], in_=log_half[:], func=ACT.Ln)

        x_codes = keep.tile([P, ROW_TILES, PASSES * P], U32, align_bytes=64)
        x_scales = keep.tile([P, ROW_TILES, PASSES * P], U8, align_bytes=64)
        l_codes = keep.tile([P, ROW_TILES, PASSES * P], U32, align_bytes=64)
        l_scales = keep.tile([P, ROW_TILES, PASSES * P], U8, align_bytes=64)

        loaded = {}
        sources = {"wh": W_hat, "mh": M_hat, "gr": gate}
        next_load = {"wh": 0, "mh": 0, "gr": 0}

        def load_columns(tag, c, n0, width):
            rows = raw.tile([P, PACK, BLOCK], BF16, tag=tag, name=tag, bufs=GATE_BUFS if tag == "gr" else RAW_BUFS)
            nc.sync.dma_start(
                out=rows[:, :, :width],
                in_=sources[tag][c * K_PASS : (c + 1) * K_PASS, n0 : n0 + width].rearrange("(p t) n -> p t n", t=PACK),
            )
            loaded.setdefault((tag, c, n0 // BLOCK), []).append((n0, width, rows))

        def load(tag, pieces=1):
            b, c = divmod(next_load[tag], PASSES)
            next_load[tag] += 1
            for q in range(pieces):
                load_columns(tag, c, b * BLOCK + q * (BLOCK // pieces), BLOCK // pieces)

        def parts(tag, piece):
            c, n0, width = piece
            res = []
            for first, w, rows in loaded[(tag, c, n0 // BLOCK)]:
                lo = max(n0, first)
                hi = min(n0 + width, first + w)
                if lo < hi:
                    res.append((lo - n0, hi - lo, rows[:, :, lo - first : hi - first]))
            return res

        def grouped(tile_, lo, width):
            return tile_[:, lo : lo + width, :].rearrange("p (c i) t -> p c t i", i=RUN)

        def words(chunk):
            return sum(width for c, n0, width in chunk)

        t1 = {}
        t2 = {}
        gg = {}
        wg = {}
        where = {}

        def tanh_pass(j, tag, scale):
            res = fac.tile([P, 2, words(W_CHUNKS[j]), 2], F32, tag="t" + tag, name="t" + tag, bufs=3 if tag == "wh" else 2)
            lo = 0
            for piece in W_CHUNKS[j]:
                for off, width, rows in parts(tag, piece):
                    nc.scalar.activation(
                        out=res[:, :, lo + off : lo + off + width, :],
                        in_=rows.rearrange("p (h u) n -> p u n h", u=2),
                        func=ACT.Tanh,
                        scale=scale,
                    )
                lo += piece[2]
            return res

        def tanh_w(j):
            t1[j] = tanh_pass(j, "wh", 1.0)

        def tanh_m(j):
            t2[j] = tanh_pass(j, "mh", 0.5)

        def w_product(j):
            wg[j] = grp.tile([P, words(W_CHUNKS[j]) * PACK], BF16, tag="wg", name="wg", align_bytes=64)
            nc.vector.scalar_tensor_tensor(
                out=wg[j][:].rearrange("p (m u) -> p m u", u=2),
                in0=t2[j][:].rearrange("p u n h -> p (n h) u"),
                scalar=1.0,
                in1=t1[j][:].rearrange("p u n h -> p (n h) u"),
                op0=ALU.add,
                op1=ALU.mult,
            )

        def quantise(kind, pool, chunk, values):
            n = words(chunk)
            cod = pool.tile([P, n], U32, tag=kind + "c", name=kind + "c", align_bytes=64)
            sca = pool.tile([P, n], U8, tag=kind + "s", name=kind + "s", align_bytes=64)
            nc.vector.quantize_mx(out=cod[:].bitcast(FP8X4), scales=sca[:], in_=values)
            lo = 0
            for c, n0, width in chunk:
                for off in range(0, width, P):
                    where[(kind, c, n0 + off)] = (cod, sca, lo + off)
                lo += width

        def w_quantise(j):
            quantise("w", wq, W_CHUNKS[j], wg[j][:])
            state["w"] = j

        def g_regroup(j):
            gg[j] = grp.tile([P, words(G_CHUNKS[j]), PACK], BF16, tag="gg", name="gg", align_bytes=64)
            lo = 0
            for piece in G_CHUNKS[j]:
                for off, width, rows in parts("gr", piece):
                    nc.vector.tensor_copy(
                        out=grouped(gg[j], lo + off, width), in_=rows.rearrange("p t (c i) -> p c t i", i=RUN)
                    )
                lo += piece[2]

        def g_quantise(j):
            quantise("g", gq, G_CHUNKS[j], gg[j][:].rearrange("p n t -> p (n t)"))
            state["g"] = j

        def product(acc, lhs_codes, lhs_scales, kind, e):
            n0, width, rows = UNITS[e]
            for q, i in enumerate(rows):
                for c in range(PASSES):
                    cod, sca, lo = where[(kind, c, n0)]
                    nc.tensor.matmul_mx(
                        out=acc[:, q * width : (q + 1) * width],
                        lhsT=lhs_codes[:, i, c * P : (c + 1) * P].bitcast(FP8X4),
                        lhsT_scale=lhs_scales[:, i, c * P : (c + 1) * P],
                        rhs=cod[:, lo : lo + width].bitcast(FP8X4),
                        rhs_scale=sca[:, lo : lo + width],
                        start=(c == 0),
                        stop=(c == PASSES - 1),
                    )

        def unit_words(e):
            return UNITS[e][1] * len(UNITS[e][2])

        W_LAST = [last_chunk(W_CHUNKS, n0) for n0, width, rows in UNITS]
        G_LAST = [last_chunk(G_CHUNKS, n0) for n0, width, rows in UNITS]
        z = {}
        s2 = {}
        a2 = {}
        state = {"z": 0, "sa": 0, "th": -1, "ex": -1, "q": -1, "w": -1, "g": -1}

        def pe_ready(w):
            go = True
            while go:
                go = False
                e = state["sa"]
                ready = []
                while len(ready) < (2 if e + 1 < len(UNITS) - 1 else 1) and e < min(len(UNITS), state["z"]) and W_LAST[e] <= w and e - 3 <= min(state["ex"], state["q"]):
                    ready.append(e)
                    e += 1
                for e in ready:
                    s2[e] = psa.tile([P, unit_words(e)], F32, tag="s", name="s")
                    product(s2[e], l_codes, l_scales, "w", e)
                for e in ready:
                    a2[e] = psa.tile([P, unit_words(e)], F32, tag="a", name="a")
                    product(a2[e], x_codes, x_scales, "w", e)
                    state["sa"] = e + 1
                    go = True
                e = state["z"]
                if e < len(UNITS) and G_LAST[e] <= state["g"] and e - 2 <= state["th"]:
                    z[e] = psz.tile([P, unit_words(e)], F32, tag="z", name="z")
                    product(z[e], x_codes, x_scales, "g", e)
                    state["z"] = e + 1
                    go = True

        with tc.tile_pool(name="xin", bufs=ROW_TILES) as xin, tc.tile_pool(name="xwork", bufs=2) as xwork:
            x_sb = {}
            x_banks = {}
            xg = {}
            lg = {}
            xgs = []
            lgs = []

            def x_load(i, pieces=1):
                x_sb[i] = xin.tile([P, IN], BF16, tag="x_sb", name="x_sb")
                n = IN // pieces
                for q in range(pieces):
                    nc.sync.dma_start(
                        out=x_sb[i][:, q * n : (q + 1) * n], in_=input_tensor[i * P : (i + 1) * P, q * n : (q + 1) * n]
                    )

            def x_transpose(i, pieces=2):
                pairs = x_sb[i][:].bitcast(F32)
                if i % 2 == 0:
                    xg_pair = xwork.tile([P, 2, PASSES * P * PACK], BF16, tag="xg", name="xg", align_bytes=64)
                    lg_pair = xwork.tile([P, 2, PASSES * P * PACK], BF16, tag="lg", name="lg", align_bytes=64)
                    for q in range(2):
                        xg[i + q] = xg_pair[:, q, :]
                        lg[i + q] = lg_pair[:, q, :]
                    xgs.append(xg_pair)
                    lgs.append(lg_pair)
                n = PASSES // pieces
                for q in range(pieces):
                    pool, tag = ((psa, "s"), (psa, "a"), (psz, "z"))[len(x_banks) % 3 if len(x_banks) < 8 else len(x_banks) % 8]
                    xt = pool.tile([P, n, 2, P], F32, tag=tag, name=tag)
                    x_banks[(i, q)] = xt
                    for c in range(q * n, (q + 1) * n):
                        for u in range(2):
                            nc.tensor.transpose(xt[:, c - q * n, u, :], pairs[:, 256 * c + u : 256 * (c + 1) : 2], ident[:])

            def x_copy(copy, i, q=0, pieces=2):
                n = PASSES // pieces
                xg_pairs = xg[i].bitcast(F32).rearrange("p (c r u) -> p c r u", c=PASSES, u=2)
                copy(out=xg_pairs[:, q * n : (q + 1) * n], in_=x_banks[(i, q)][:].rearrange("p c u r -> p c r u"))

            def flat(ap):
                return ap.rearrange("p i n -> p (i n)")

            def x_quantise(h):
                two = slice(2 * h, 2 * h + 2)
                nc.vector.quantize_mx(
                    out=flat(x_codes[:, two, :]).bitcast(FP8X4), scales=flat(x_scales[:, two, :]), in_=flat(xgs[h][:])
                )

            def x_abs(i, q=0, pieces=1):
                n = PASSES * P * PACK // pieces
                part = slice(q * n // 2, (q + 1) * n // 2)
                nc.vector.tensor_single_scalar(
                    out=lg[i].bitcast(I32)[:, part], in_=xg[i].bitcast(I32)[:, part], scalar=0x7FFF7FFF, op=ALU.bitwise_and
                )

            def x_log(i, q=0, pieces=1):
                n = PASSES * P * PACK // pieces
                part = lg[i][:, q * n : (q + 1) * n]
                nc.scalar.activation(out=part, in_=part, func=ACT.Ln, bias=eps[:], scale=1.0)

            def l_quantise(h):
                two = slice(2 * h, 2 * h + 2)
                nc.vector.quantize_mx(
                    out=flat(l_codes[:, two, :]).bitcast(FP8X4), scales=flat(l_scales[:, two, :]), in_=flat(lgs[h][:])
                )

            x_load(0, 4)
            for item in HEAD_LOADS:
                if item in ("gr", "wh", "mh"):
                    load(item)
                else:
                    x_load(int(item), 2 if item == "1" else 1)
            vec = nc.vector.tensor_copy
            sca = nc.scalar.copy
            for i in range(ROW_TILES):
                x_transpose(i, 4 if i == 0 else 2)
            x_copy(vec, 0, 0, 4)
            x_copy(vec, 0, 1, 4)
            x_abs(0, 0, 4)
            x_copy(vec, 0, 2, 4)
            x_abs(0, 1, 4)
            x_copy(vec, 0, 3, 4)
            x_abs(0, 2, 4)
            x_abs(0, 3, 4)
            x_copy(vec, 1, 0, 2)
            x_copy(vec, 1, 1, 2)
            x_abs(1, 0, 2)
            x_abs(1, 1, 2)
            x_quantise(0)
            g_regroup(0)
            x_log(0, 0, 4)
            x_log(0, 1, 4)
            x_log(0, 2, 4)
            x_log(0, 3, 4)
            x_log(1, 0, 2)
            x_copy(sca, 2, 0, 2)
            x_copy(sca, 2, 1, 2)
            x_abs(2, 0, 1)
            g_quantise(0)
            x_copy(vec, 3, 0, 2)
            g_regroup(1)
            x_log(1, 1, 2)
            x_copy(sca, 3, 1, 2)
            x_abs(3, 0, 1)
            x_quantise(1)
            g_quantise(1)
            l_quantise(0)
            g_regroup(2)
            x_log(2, 0, 1)
            x_log(3, 0, 1)
            l_quantise(1)
            g_regroup(3)
            g_quantise(2)
            g_quantise(3)


        wq = ctx.enter_context(tc.tile_pool(name="wq", bufs=WQ_BUFS))
        epi = ctx.enter_context(tc.tile_pool(name="epi", bufs=3))
        outs = ctx.enter_context(tc.tile_pool(name="outs", bufs=5))
        gates = ctx.enter_context(tc.tile_pool(name="gates", bufs=6))
        th = {}
        m = {}
        ga = {}

        def gate_tanh(e):
            th[e] = gates.tile([P, unit_words(e)], F32, tag="th", name="th")
            nc.scalar.activation(out=th[e][:], in_=z[e][:], func=ACT.Tanh, scale=0.5)
            state["th"] = e

        def exp(e):
            m[e] = outs.tile([P, unit_words(e)], F32, tag="m", name="m")
            nc.scalar.activation(out=m[e][:], in_=s2[e][:], func=ACT.Exp, bias=log_half[:], scale=0.5)
            state["ex"] = e

        def blend_q(e):
            ga[e] = epi.tile([P, unit_words(e)], F32, tag="ga", name="ga")
            nc.vector.scalar_tensor_tensor(out=ga[e][:], in0=th[e][:], scalar=1.0, in1=a2[e][:], op0=ALU.add, op1=ALU.mult)
            state["q"] = e

        def blend_r(e):
            nc.vector.scalar_tensor_tensor(out=m[e][:], in0=th[e][:], scalar=1.0, in1=m[e][:], op0=ALU.subtract, op1=ALU.mult)

        def blend_o(e):
            n0, width, rows = UNITS[e]
            nc.vector.scalar_tensor_tensor(out=m[e][:], in0=ga[e][:], scalar=0.25, in1=m[e][:], op0=ALU.mult, op1=ALU.subtract)
            nc.sync.dma_start(
                out=out[rows[0] * P : (rows[-1] + 1) * P, n0 : n0 + width].rearrange("(i p) n -> p i n", p=P),
                in_=m[e][:].rearrange("p (i n) -> p i n", n=width),
            )

        pe_ready(-1)
        EX_AT = {}
        TH_AT = {}
        place = th_place = 0
        issued = []
        for chunk in W_CHUNKS:
            for half in range(2):
                issued.append((issued[-1] if issued else 0) + words(chunk))
        for e in range(len(UNITS)):
            place = max(place + EX_STEP, 2 * (W_LAST[e] + 1) + 1)
            while place < len(issued) and issued[place] - issued[2 * W_LAST[e] + 1] < EX_LAG:
                place += 1
            EX_AT.setdefault(place, []).append(e)
            th_place = max(th_place + 1, place - TH_LEAD)
            TH_AT.setdefault(th_place, []).append(e)
        last_use = {}
        for j, chunk in enumerate(W_CHUNKS):
            for c, n0, width in chunk:
                last_use[n0 // BLOCK * PASSES + c] = j
        n_loads = OUT // BLOCK * PASSES
        gates_done = HEAD_GATES
        late = []
        def load_ahead(j):
            go = True
            while go:
                go = False
                if next_load["wh"] < n_loads and (next_load["wh"] < RAW_BUFS or last_use[next_load["wh"] - RAW_BUFS] <= j):
                    load("wh")
                    load("mh")
                    go = True
                if next_load["gr"] < min(n_loads, gates_done + GATE_BUFS):
                    load("gr")
                    go = True

        load_ahead(-1)
        for j in range(len(W_CHUNKS)):
            tanh_w(j)
            for e in TH_AT.get(2 * j, ()):
                gate_tanh(e)
                pe_ready(j - 2)
            for e in EX_AT.get(2 * j, ()):
                exp(e)
            tanh_m(j)
            for e in TH_AT.get(2 * j + 1, ()):
                gate_tanh(e)
                pe_ready(j - 2)
            pe_ready(j - 1)
            for e in EX_AT.get(2 * j + 1, ()):
                exp(e)
            units = EX_AT.get(2 * j, []) + EX_AT.get(2 * j + 1, [])
            fresh = range(gates_done, min(len(G_CHUNKS), gates_done + 1))
            gates_done += len(fresh)
            ops = [(blend_o, e) for e in late] + [(g_regroup, g) for g in fresh] + [(blend_q, e) for e in units]
            ops += [(w_product, j)] + [(blend_r, e) for e in units] + [(g_quantise, g) for g in fresh] + [(w_quantise, j)]
            late = units
            for op, which in ops:
                op(which)
                pe_ready(j - 1)
            load_ahead(j)
        for e in late:
            blend_o(e)
        first = state["ex"] + 1
        for e in range(first, len(UNITS)):
            pe_ready(len(W_CHUNKS) - 2)
            if state["th"] < e:
                gate_tanh(e)
            pe_ready(state["w"])
            exp(e)
            blend_r(e)
            if e > first:
                blend_o(e - 1)
            blend_q(e)
        blend_o(len(UNITS) - 1)
